import numpy as np
import ml_dtypes


def mxq(x, axis, fmt="e4m3"):
    dtype, down = {"e4m3": (ml_dtypes.float8_e4m3fn, 7), "e5m2": (ml_dtypes.float8_e5m2, 14)}[fmt]
    v = np.moveaxis(np.asarray(x, np.float32).astype(ml_dtypes.bfloat16).astype(np.float64), axis, -1)
    blocks = v.reshape(v.shape[:-1] + (-1, 32))
    amax = np.abs(blocks).max(-1, keepdims=True)
    byte = np.maximum(np.where(amax > 0, np.frexp(amax)[1] - 1 + 127, 0) - down, 1)
    scale = np.exp2(byte - 127.0)
    codes = (blocks / scale).astype(np.float32).astype(dtype).astype(np.float64)
    return np.moveaxis((codes * scale).reshape(v.shape), -1, axis)


WIDE = False


def mx_kscale(k):
    if not WIDE:
        return np.ones(k)
    levels = np.array([10, -10, 5, -5, 0])
    a = np.random.permutation(np.resize(levels, k // 512 * 4)).reshape(k // 512, 4)
    idx = np.arange(k)
    return np.exp2(a[idx // 512, idx % 128 // 32])


BF16 = ml_dtypes.bfloat16


def bf(x):
    return np.asarray(x, np.float32).astype(BF16)


def f64(x):
    return np.asarray(x).astype(np.float64)


B, O, D, G1, G2, F1, F2 = 64, 8, 512, 512, 512, 512, 512
C = D + D
P = O * O


def setup_inputs():
    s = mx_kscale(C)[:D]
    ss = np.concatenate([s, s])
    t = mx_kscale(G1)
    return {
        "objs": bf(np.random.standard_normal((B, O, D)) * s),
        "W1": bf(np.random.standard_normal((G1, C)) / np.sqrt(C) / ss * t[:, None]),
        "b1": bf(np.random.standard_normal(G1) * 0.3 * t),
        "W2": bf(np.random.standard_normal((G2, G1)) * 0.5 / np.sqrt(G1) / t),
        "b2": bf(np.random.standard_normal(G2) * 0.15),
    }


def reference(objs, W1, b1, W2, b2):
    v = f64(objs)
    v_i = np.broadcast_to(v[:, None, :, :], (B, O, O, D))
    v_j = np.broadcast_to(v[:, :, None, :], (B, O, O, D))
    pairs = np.concatenate([v_i, v_j], axis=-1).reshape(B, P, C)
    h = np.maximum((mxq(pairs, 2, "e4m3") @ mxq(f64(W1).T, 0, "e4m3")) + f64(b1), 0.0)
    x_pairs = np.maximum((mxq(h, 2, "e4m3") @ mxq(f64(W2).T, 0, "e4m3")) + f64(b2), 0.0)
    return x_pairs, x_pairs.sum(axis=1)

@@ -1,0 +1,285 @@
+import concourse.mybir as mybir
+from concourse.masks import make_identity
+
+F32 = mybir.dt.float32
+BF16 = mybir.dt.bfloat16
+U32 = mybir.dt.uint32
+U8 = mybir.dt.uint8
+FP8X4 = mybir.dt.float8_e4m3fn_x4
+ADD = mybir.AluOpType.add
+MAX = mybir.AluOpType.max
+MIN = mybir.AluOpType.min
+RELU = mybir.ActivationFunctionType.Relu
+
+P = 128
+NB = 64
+NO = 8
+D = 512
+G1 = 512
+G2 = 512
+FLOPS = 2 * NB * NO * NO * (2 * D) * G1 + 2 * NB * NO * NO * G1 * G2
+
+GB = 8
+NGRP = NB // GB
+SELW = 64
+SREG = 126
+G_GROUPS = ()
+RES_Q = (0, 2)
+BIG = 3.3895313892515355e38
+GPIECE = 2
+
+
+def body(tc, objs, W1, b1, W2, b2, out_0, out_1, const, ps, pres):
+    nc = tc.nc
+    b1t = const.tile([P, 2, 2], BF16)
+    nc.scalar.dma_start(out=b1t[:], in_=b1.rearrange("(u p e) -> p u e", u=2, e=2))
+    bz = const.tile([P, G2], BF16)
+    nc.vector.memset(bz[:], 0.0)
+    nc.scalar.dma_start(out=bz[0:1, :], in_=b2.rearrange("(o n) -> o n", o=1))
+    objs_sb = const.tile([P, 4, D], BF16)
+    nc.sync.dma_start(out=objs_sb[:], in_=objs.rearrange("b o d -> (b o) d").rearrange("(r p) d -> p r d", p=P))
+    w1_sb = const.tile([P, 4, 2 * D], BF16)
+    w1v = W1.rearrange("(u p e) c -> u p e c", u=2, e=2)
+    for u in range(2):
+        nc.sync.dma_start(out=w1_sb[:, 2 * u : 2 * u + 2, :], in_=w1v[u])
+    w2_sb = const.tile([P, 4, G1], BF16)
+    nc.sync.dma_start(out=w2_sb[:], in_=W2.rearrange("(j p) c -> p j c", p=P))
+
+    ident = const.tile([P, P], F32)
+    make_identity(nc, ident[:])
+    ones = const.tile([P, P], BF16)
+    nc.vector.memset(ones[:], 1.0)
+    sel = const.tile([P, SELW], F32)
+    nc.vector.memset(sel[:], 0.0)
+    nc.vector.memset(sel[0:64, 0:1], 1.0)
+    nc.vector.memset(sel[64:128, 1:2], 1.0)
+
+    def flip(src_sb, g, h, grouped, eng):
+        gw = grouped.bitcast(F32).rearrange("p (c u) -> p c u", u=2)
+        bank = ps.tile([P, 512], F32, tag="work", name="fl")
+        for rt in range(2):
+            words = src_sb[:, 2 * h + rt, :].bitcast(F32)
+            for u in range(2):
+                nc.tensor.transpose(
+                    bank[:, (2 * rt + u) * P : (2 * rt + u + 1) * P],
+                    words[:, 256 * g + P * u : 256 * g + P * u + P],
+                    ident[:],
+                )
+        dst = gw[:, 256 * h : 256 * h + 256, :].rearrange("p (rt c) u -> p rt c u", rt=2)
+        src = bank[:].rearrange("p (rt u c) -> p rt c u", rt=2, u=2)
+        if eng == "s":
+            nc.scalar.copy(out=dst, in_=src)
+        else:
+            nc.vector.tensor_copy(out=dst, in_=src)
+
+    def quant(codes, scales, grouped, h):
+        nc.vector.quantize_mx(
+            out=codes[:, 256 * h : 256 * h + 256].bitcast(FP8X4),
+            scales=scales[:, 256 * h : 256 * h + 256],
+            in_=grouped[:, 1024 * h : 1024 * h + 1024],
+        )
+
+    og = const.tile([P, 2048], BF16, align_bytes=64)
+    oc = const.tile([P, 512], U32, align_bytes=64)
+    osc = const.tile([P, 512], U8, align_bytes=64)
+    w1g = [const.tile([P, 2048], BF16, align_bytes=64, name="w1g%d" % g) for g in range(2)]
+    w1c = [const.tile([P, 512], U32, align_bytes=64, name="w1c%d" % g) for g in range(2)]
+    w1s = [const.tile([P, 512], U8, align_bytes=64, name="w1s%d" % g) for g in range(2)]
+    w2g = const.tile([P, 2048], BF16, align_bytes=64)
+    w2c = const.tile([P, 512], U32, align_bytes=64)
+    w2s = const.tile([P, 512], U8, align_bytes=64)
+
+    flip(objs_sb, 0, 0, og[:], "s")
+    flip(objs_sb, 0, 1, og[:], "v")
+    flip(w1_sb, 0, 0, w1g[0][:], "s")
+    quant(oc, osc, og, 0)
+    quant(oc, osc, og, 1)
+    flip(w1_sb, 1, 0, w1g[1][:], "v")
+    quant(w1c[0], w1s[0], w1g[0], 0)
+    flip(w1_sb, 0, 1, w1g[0][:], "s")
+    quant(w1c[1], w1s[1], w1g[1], 0)
+    flip(w1_sb, 1, 1, w1g[1][:], "v")
+    quant(w1c[0], w1s[0], w1g[0], 1)
+    quant(w1c[1], w1s[1], w1g[1], 1)
+
+    a_sb = const.tile([P, NB, NO, 4], F32)
+    b_sb = const.tile([P, NB, NO, 4], F32)
+    b1b = b1t[:].rearrange("p u e -> p (u e)").unsqueeze(1).to_broadcast([P, P, 4])
+    bres = {}
+
+    def layer1(q):
+        for g in range(2):
+            if g == 1 and q in RES_Q:
+                bank = pres.tile([P, 512], F32, name="bres%d" % q)
+                bres[q] = bank
+            else:
+                bank = ps.tile([P, 512], F32, tag="work", name="l1")
+            for t in range(4):
+                nc.tensor.matmul_mx(
+                    out=bank[:, P * t : P * t + P],
+                    lhsT=w1c[g][:, P * t : P * t + P].bitcast(FP8X4),
+                    lhsT_scale=w1s[g][:, P * t : P * t + P],
+                    rhs=oc[:, P * q : P * q + P].bitcast(FP8X4),
+                    rhs_scale=osc[:, P * q : P * q + P],
+                    start=True,
+                    stop=True,
+                )
+            src = bank[:].rearrange("p (t c) -> p c t", t=4)
+            if g == 0:
+                nc.vector.tensor_tensor(
+                    out=a_sb[:, 16 * q : 16 * q + 16, :, :].rearrange("p b m t -> p (b m) t"), in0=src, in1=b1b, op=ADD
+                )
+            elif q not in RES_Q:
+                nc.scalar.copy(out=b_sb[:, 16 * q : 16 * q + 16, :, :].rearrange("p b m t -> p (b m) t"), in_=src)
+
+    hp = [const.tile([P, 2048], BF16, align_bytes=64, name="hp%d" % n) for n in range(NGRP)]
+    hc = [const.tile([P, 512], U32, align_bytes=64, name="hc%d" % n) for n in range(NGRP)]
+    hs = [const.tile([P, 512], U8, align_bytes=64, name="hs%d" % n) for n in range(NGRP)]
+    xg = [const.tile([P, 4, G2], F32, name="xg%d" % n) for n in range(NGRP)]
+    zt = {}
+    st = pres.tile([P, 512], F32)
+    out0v = out_0.rearrange("b q g -> (b q) g").rearrange("(n j p) g -> n p j g", j=4, p=P)
+
+    def ok(n):
+        return 0 <= n < NGRP
+
+    def t1(n):
+        if not ok(n) or n in G_GROUPS:
+            return
+        q = n // 2
+        shape5 = [P, GB, NO, NO, 4]
+        b0 = GB * n
+        if q in RES_Q:
+            in1 = bres[q][:].rearrange("p (t b k) -> p b k t", t=4, b=16)[:, GB * (n % 2) : GB * (n % 2) + GB, :, :]
+        else:
+            in1 = b_sb[:, b0 : b0 + GB, :, :]
+        nc.vector.tensor_tensor(
+            out=hp[n][:].rearrange("p (b k m t) -> p b k m t", b=GB, k=NO, m=NO),
+            in0=a_sb[:, b0 : b0 + GB, :, :].unsqueeze(2).to_broadcast(shape5),
+            in1=in1.unsqueeze(3).to_broadcast(shape5),
+            op=ADD,
+        )
+
+    def t1g(n):
+        if n not in G_GROUPS:
+            return
+        shape5 = [P, GPIECE, NO, NO, 4]
+        w = GPIECE * 256
+        for i in range(GB // GPIECE):
+            b0 = GB * n + GPIECE * i
+            piece = hp[n][:, w * i : w * i + w]
+            nc.gpsimd.tensor_tensor(
+                out=piece.rearrange("p (b k m t) -> p b k m t", b=GPIECE, k=NO, m=NO),
+                in0=a_sb[:, b0 : b0 + GPIECE, :, :].unsqueeze(2).to_broadcast(shape5),
+                in1=b_sb[:, b0 : b0 + GPIECE, :, :].unsqueeze(3).to_broadcast(shape5),
+                op=ADD,
+            )
+            nc.gpsimd.tensor_scalar(out=piece, in0=piece, scalar1=BIG, scalar2=0.0, op0=MIN, op1=MAX)
+
+    def t2(n):
+        if not ok(n) or n in G_GROUPS:
+            return
+        nc.scalar.activation(out=hp[n][:], in_=hp[n][:], func=RELU)
+
+    def t3(n):
+        if not ok(n):
+            return
+        nc.vector.quantize_mx(out=hc[n][:].bitcast(FP8X4), scales=hs[n][:], in_=hp[n][:])
+
+    def l2(n, j):
+        if not ok(n):
+            return
+        z = ps.tile([P, 512], F32, tag="work", name="z")
+        zt[(n, j)] = z
+        nc.tensor.matmul_mx(
+            out=z[:],
+            lhsT=hc[n][:, P * j : P * j + P].bitcast(FP8X4),
+            lhsT_scale=hs[n][:, P * j : P * j + P],
+            rhs=w2c[:].bitcast(FP8X4),
+            rhs_scale=w2s[:],
+            start=True,
+            stop=True,
+        )
+
+    def t4(n, j):
+        if not ok(n):
+            return
+        nc.vector.tensor_tensor(out=xg[n][:, j, :], in0=zt[(n, j)][:], in1=b2bc[:], op=ADD)
+
+    def t5(n, j0, j1):
+        if not ok(n):
+            return
+        nc.scalar.activation(out=xg[n][:, j0:j1, :], in_=xg[n][:, j0:j1, :], func=RELU)
+        nc.sync.dma_start(out=out0v[n][:, j0:j1, :], in_=xg[n][:, j0:j1, :])
+
+    def sm(n, j):
+        if not ok(n):
+            return
+        tl = 4 * n + j
+        for c in range(4):
+            nc.tensor.matmul(
+                out=st[:, SREG * c + 2 * tl : SREG * c + 2 * tl + SELW],
+                lhsT=xg[n][:, j, P * c : P * c + P],
+                rhs=sel[:],
+                start=True,
+                stop=True,
+            )
+
+    layer1(0)
+    flip(w2_sb, 0, 0, w2g[:], "s")
+    flip(w2_sb, 0, 1, w2g[:], "s")
+    b2ps = ps.tile([P, 512], F32, tag="work")
+    nc.tensor.matmul(out=b2ps[:], lhsT=ones[:], rhs=bz[:], start=True, stop=True)
+    b2bc = const.tile([P, G2], F32)
+    nc.scalar.copy(out=b2bc[:], in_=b2ps[:])
+    t1(0)
+    layer1(1)
+    t2(0)
+    t1g(2)
+    t1g(3)
+    quant(w2c, w2s, w2g, 0)
+    quant(w2c, w2s, w2g, 1)
+    t1(1)
+    layer1(2)
+    layer1(3)
+    t1g(6)
+    t1g(7)
+
+    last = NGRP - 1
+    for i in range(-1, NGRP):
+        t3(i + 1)
+        l2(i + 1, 0)
+        for j in range(4):
+            sm(i - 1, j)
+        t2(i + 2)
+        for j in range(4):
+            t4(i, j)
+            if j < 3:
+                l2(i + 1, j + 1)
+            if i == last:
+                t5(i, j, j + 1)
+                sm(i, j)
+            elif j % 2 == 1:
+                t5(i, j - 1, j + 1)
+        t1(i + 3)
+
+    sts = const.tile([P, 4, NB], F32)
+    nc.vector.tensor_copy(out=sts[:], in_=st[:, 0 : 4 * SREG].rearrange("p (c w) -> p c w", c=4)[:, :, 0:NB])
+    fin = ps.tile([P, 512], F32, tag="work")
+    for cp in range(2):
+        nc.tensor.transpose(
+            fin[:, P * cp : P * cp + P], sts[:, 2 * cp : 2 * cp + 2, :].rearrange("p a b -> p (a b)"), ident[:]
+        )
+    s_sb = const.tile([P, 2, P], F32)
+    nc.vector.tensor_copy(out=s_sb[:].rearrange("p a g -> p (a g)"), in_=fin[:, 0 : 2 * P])
+    out1v = out_1.rearrange("b (cp cc g) -> cc b cp g", cp=2, cc=2)
+    for cc in range(2):
+        nc.sync.dma_start(out=out1v[cc], in_=s_sb[64 * cc : 64 * cc + 64, :, :])
+
+
+def tile_pairwiserelationmodule_pa_kernel(tc, objs, W1, b1, W2, b2, out_0, out_1):
+    with tc.tile_pool(name="const", bufs=1) as const, tc.psum_pool(name="ps", bufs=5) as ps, tc.psum_pool(
+        name="pres", bufs=1
+    ) as pres:
+        with tc.manual_schedule():
+            body(tc, objs, W1, b1, W2, b2, out_0, out_1, const, ps, pres)

@@ -21,10 +21,10 @@ FLOPS = 2 * NB * NO * NO * (2 * D) * G1 + 2 * NB * NO * NO * G1 * G2
 
 GB = 8
 NGRP = NB // GB
-SELW = 64
-SREG = 126
-G_GROUPS = ()
-RES_Q = (0, 2)
+SELW = 32
+SREG = 94
+G_GROUPS = (4, 5, 6, 7)
+RES_Q = (0, 1)
 BIG = 3.3895313892515355e38
 GPIECE = 2
 
@@ -37,11 +37,13 @@ def body(tc, objs, W1, b1, W2, b2, out_0, out_1, const, ps, pres):
     nc.vector.memset(bz[:], 0.0)
     nc.scalar.dma_start(out=bz[0:1, :], in_=b2.rearrange("(o n) -> o n", o=1))
     objs_sb = const.tile([P, 4, D], BF16)
-    nc.sync.dma_start(out=objs_sb[:], in_=objs.rearrange("b o d -> (b o) d").rearrange("(r p) d -> p r d", p=P))
+    objv = objs.rearrange("b o d -> (b o) d").rearrange("(r p) d -> p r d", p=P)
     w1_sb = const.tile([P, 4, 2 * D], BF16)
     w1v = W1.rearrange("(u p e) c -> u p e c", u=2, e=2)
-    for u in range(2):
-        nc.sync.dma_start(out=w1_sb[:, 2 * u : 2 * u + 2, :], in_=w1v[u])
+    for g in range(2):
+        nc.sync.dma_start(out=objs_sb[:, 2 * g : 2 * g + 2, :], in_=objv[:, 2 * g : 2 * g + 2, :])
+        for u in range(2):
+            nc.sync.dma_start(out=w1_sb[:, 2 * u : 2 * u + 2, D * g : D * g + D], in_=w1v[u][:, :, D * g : D * g + D])
     w2_sb = const.tile([P, 4, G1], BF16)
     nc.sync.dma_start(out=w2_sb[:], in_=W2.rearrange("(j p) c -> p j c", p=P))
 
@@ -90,16 +92,16 @@ def body(tc, objs, W1, b1, W2, b2, out_0, out_1, const, ps, pres):
     w2s = const.tile([P, 512], U8, align_bytes=64)
 
     flip(objs_sb, 0, 0, og[:], "s")
-    flip(objs_sb, 0, 1, og[:], "v")
     flip(w1_sb, 0, 0, w1g[0][:], "s")
+    flip(w1_sb, 0, 1, w1g[0][:], "v")
     quant(oc, osc, og, 0)
-    quant(oc, osc, og, 1)
-    flip(w1_sb, 1, 0, w1g[1][:], "v")
+    flip(objs_sb, 0, 1, og[:], "s")
     quant(w1c[0], w1s[0], w1g[0], 0)
-    flip(w1_sb, 0, 1, w1g[0][:], "s")
-    quant(w1c[1], w1s[1], w1g[1], 0)
-    flip(w1_sb, 1, 1, w1g[1][:], "v")
     quant(w1c[0], w1s[0], w1g[0], 1)
+    flip(w1_sb, 1, 0, w1g[1][:], "s")
+    flip(w1_sb, 1, 1, w1g[1][:], "v")
+    quant(oc, osc, og, 1)
+    quant(w1c[1], w1s[1], w1g[1], 0)
     quant(w1c[1], w1s[1], w1g[1], 1)
 
     a_sb = const.tile([P, NB, NO, 4], F32)
@@ -226,21 +228,21 @@ def body(tc, objs, W1, b1, W2, b2, out_0, out_1, const, ps, pres):
             )
 
     layer1(0)
+    layer1(2)
+    t1g(4)
+    t1g(5)
+    t1(0)
     flip(w2_sb, 0, 0, w2g[:], "s")
     flip(w2_sb, 0, 1, w2g[:], "s")
     b2ps = ps.tile([P, 512], F32, tag="work")
     nc.tensor.matmul(out=b2ps[:], lhsT=ones[:], rhs=bz[:], start=True, stop=True)
     b2bc = const.tile([P, G2], F32)
     nc.scalar.copy(out=b2bc[:], in_=b2ps[:])
-    t1(0)
-    layer1(1)
     t2(0)
-    t1g(2)
-    t1g(3)
     quant(w2c, w2s, w2g, 0)
     quant(w2c, w2s, w2g, 1)
     t1(1)
-    layer1(2)
+    layer1(1)
     layer1(3)
     t1g(6)
     t1g(7)
@@ -249,8 +251,8 @@ def body(tc, objs, W1, b1, W2, b2, out_0, out_1, const, ps, pres):
     for i in range(-1, NGRP):
         t3(i + 1)
         l2(i + 1, 0)
-        for j in range(4):
-            sm(i - 1, j)
+        sm(i - 1, 2)
+        sm(i - 1, 3)
         t2(i + 2)
         for j in range(4):
             t4(i, j)
@@ -261,6 +263,9 @@ def body(tc, objs, W1, b1, W2, b2, out_0, out_1, const, ps, pres):
                 sm(i, j)
             elif j % 2 == 1:
                 t5(i, j - 1, j + 1)
+        if i != last:
+            sm(i, 0)
+            sm(i, 1)
         t1(i + 3)
 
     sts = const.tile([P, 4, NB], F32)

@@ -7,9 +7,8 @@ U32 = mybir.dt.uint32
 U8 = mybir.dt.uint8
 FP8X4 = mybir.dt.float8_e4m3fn_x4
 ADD = mybir.AluOpType.add
-MAX = mybir.AluOpType.max
-MIN = mybir.AluOpType.min
 RELU = mybir.ActivationFunctionType.Relu
+AXX = mybir.AxisListType.X
 
 P = 128
 NB = 64
@@ -18,18 +17,11 @@ D = 512
 G1 = 512
 G2 = 512
 FLOPS = 2 * NB * NO * NO * (2 * D) * G1 + 2 * NB * NO * NO * G1 * G2
-
-GB = 8
-NGRP = NB // GB
-SELW = 32
-SREG = 94
-G_GROUPS = (4, 5, 6, 7)
-RES_Q = (0, 1)
-BIG = 3.3895313892515355e38
-GPIECE = 2
+NGRP = 8
+NT = 32
 
 
-def body(tc, objs, W1, b1, W2, b2, out_0, out_1, const, ps, pres):
+def body(tc, objs, W1, b1, W2, b2, out_0, out_1, const, ps, pacc):
     nc = tc.nc
     b1t = const.tile([P, 2, 2], BF16)
     nc.scalar.dma_start(out=b1t[:], in_=b1.rearrange("(u p e) -> p u e", u=2, e=2))
@@ -40,8 +32,8 @@ def body(tc, objs, W1, b1, W2, b2, out_0, out_1, const, ps, pres):
     objv = objs.rearrange("b o d -> (b o) d").rearrange("(r p) d -> p r d", p=P)
     w1_sb = const.tile([P, 4, 2 * D], BF16)
     w1v = W1.rearrange("(u p e) c -> u p e c", u=2, e=2)
+    nc.sync.dma_start(out=objs_sb[:], in_=objv)
     for g in range(2):
-        nc.sync.dma_start(out=objs_sb[:, 2 * g : 2 * g + 2, :], in_=objv[:, 2 * g : 2 * g + 2, :])
         for u in range(2):
             nc.sync.dma_start(out=w1_sb[:, 2 * u : 2 * u + 2, D * g : D * g + D], in_=w1v[u][:, :, D * g : D * g + D])
     w2_sb = const.tile([P, 4, G1], BF16)
@@ -51,14 +43,18 @@ def body(tc, objs, W1, b1, W2, b2, out_0, out_1, const, ps, pres):
     make_identity(nc, ident[:])
     ones = const.tile([P, P], BF16)
     nc.vector.memset(ones[:], 1.0)
-    sel = const.tile([P, SELW], F32)
-    nc.vector.memset(sel[:], 0.0)
-    nc.vector.memset(sel[0:64, 0:1], 1.0)
-    nc.vector.memset(sel[64:128, 1:2], 1.0)
+
+    nbank = [0]
+
+    def head_bank():
+        nbank[0] += 1
+        if nbank[0] % 2 == 0:
+            return pacc.tile([P, 512], F32, tag="acc", name="hb")
+        return ps.tile([P, 512], F32, tag="work", name="hw")
 
     def flip(src_sb, g, h, grouped, eng):
         gw = grouped.bitcast(F32).rearrange("p (c u) -> p c u", u=2)
-        bank = ps.tile([P, 512], F32, tag="work", name="fl")
+        bank = head_bank()
         for rt in range(2):
             words = src_sb[:, 2 * h + rt, :].bitcast(F32)
             for u in range(2):
@@ -92,101 +88,80 @@ def body(tc, objs, W1, b1, W2, b2, out_0, out_1, const, ps, pres):
     w2s = const.tile([P, 512], U8, align_bytes=64)
 
     flip(objs_sb, 0, 0, og[:], "s")
+    flip(objs_sb, 0, 1, og[:], "v")
     flip(w1_sb, 0, 0, w1g[0][:], "s")
-    flip(w1_sb, 0, 1, w1g[0][:], "v")
     quant(oc, osc, og, 0)
-    flip(objs_sb, 0, 1, og[:], "s")
+    flip(w1_sb, 0, 1, w1g[0][:], "v")
+    quant(oc, osc, og, 1)
     quant(w1c[0], w1s[0], w1g[0], 0)
     quant(w1c[0], w1s[0], w1g[0], 1)
     flip(w1_sb, 1, 0, w1g[1][:], "s")
     flip(w1_sb, 1, 1, w1g[1][:], "v")
-    quant(oc, osc, og, 1)
     quant(w1c[1], w1s[1], w1g[1], 0)
     quant(w1c[1], w1s[1], w1g[1], 1)
 
-    a_sb = const.tile([P, NB, NO, 4], F32)
-    b_sb = const.tile([P, NB, NO, 4], F32)
-    b1b = b1t[:].rearrange("p u e -> p (u e)").unsqueeze(1).to_broadcast([P, P, 4])
-    bres = {}
+    a2 = const.tile([P, NO, NB, 2, 4], F32)
+    bk = const.tile([P, 4, NB, 2, 4], F32)
+    b1b = b1t[:].rearrange("p u e -> p (u e)").unsqueeze(1).unsqueeze(1).to_broadcast([P, NO, 16, 4])
 
-    def layer1(q):
-        for g in range(2):
-            if g == 1 and q in RES_Q:
-                bank = pres.tile([P, 512], F32, name="bres%d" % q)
-                bres[q] = bank
-            else:
-                bank = ps.tile([P, 512], F32, tag="work", name="l1")
-            for t in range(4):
-                nc.tensor.matmul_mx(
-                    out=bank[:, P * t : P * t + P],
-                    lhsT=w1c[g][:, P * t : P * t + P].bitcast(FP8X4),
-                    lhsT_scale=w1s[g][:, P * t : P * t + P],
-                    rhs=oc[:, P * q : P * q + P].bitcast(FP8X4),
-                    rhs_scale=osc[:, P * q : P * q + P],
-                    start=True,
-                    stop=True,
-                )
-            src = bank[:].rearrange("p (t c) -> p c t", t=4)
-            if g == 0:
-                nc.vector.tensor_tensor(
-                    out=a_sb[:, 16 * q : 16 * q + 16, :, :].rearrange("p b m t -> p (b m) t"), in0=src, in1=b1b, op=ADD
-                )
-            elif q not in RES_Q:
-                nc.scalar.copy(out=b_sb[:, 16 * q : 16 * q + 16, :, :].rearrange("p b m t -> p (b m) t"), in_=src)
+    def mx1(g, q):
+        bank = head_bank()
+        for t in range(4):
+            nc.tensor.matmul_mx(
+                out=bank[:, P * t : P * t + P],
+                lhsT=w1c[g][:, P * t : P * t + P].bitcast(FP8X4),
+                lhsT_scale=w1s[g][:, P * t : P * t + P],
+                rhs=oc[:, P * q : P * q + P].bitcast(FP8X4),
+                rhs_scale=osc[:, P * q : P * q + P],
+                start=True,
+                stop=True,
+            )
+        return bank
+
+    def layer1a(q):
+        bank = mx1(0, q)
+        bs = slice(16 * q, 16 * q + 16)
+        nc.vector.tensor_tensor(
+            out=a2[:, :, bs, 0, :], in0=bank[:].rearrange("p (t b m) -> p m b t", t=4, b=16), in1=b1b, op=ADD
+        )
+        nc.scalar.copy(out=a2[:, :, bs, 1, :], in_=a2[:, :, bs, 0, :])
+
+    def layer1b(q):
+        bank = mx1(1, q)
+        bs = slice(16 * q, 16 * q + 16)
+        src = bank[:].rearrange("p (t b kh kl) -> p kh kl b t", t=4, b=16, kh=2)
+        for kh in range(2):
+            nc.scalar.copy(out=bk[:, :, bs, kh, :], in_=src[:, kh])
 
     hp = [const.tile([P, 2048], BF16, align_bytes=64, name="hp%d" % n) for n in range(NGRP)]
     hc = [const.tile([P, 512], U32, align_bytes=64, name="hc%d" % n) for n in range(NGRP)]
     hs = [const.tile([P, 512], U8, align_bytes=64, name="hs%d" % n) for n in range(NGRP)]
     xg = [const.tile([P, 4, G2], F32, name="xg%d" % n) for n in range(NGRP)]
     zt = {}
-    st = pres.tile([P, 512], F32)
-    out0v = out_0.rearrange("b q g -> (b q) g").rearrange("(n j p) g -> n p j g", j=4, p=P)
+    acc = []
+    out0v = out_0.rearrange("b q g -> (b q) g").rearrange("(p t) g -> p t g", t=NT)
 
     def ok(n):
         return 0 <= n < NGRP
 
     def t1(n):
-        if not ok(n) or n in G_GROUPS:
+        if not ok(n):
             return
-        q = n // 2
-        shape5 = [P, GB, NO, NO, 4]
-        b0 = GB * n
-        if q in RES_Q:
-            in1 = bres[q][:].rearrange("p (t b k) -> p b k t", t=4, b=16)[:, GB * (n % 2) : GB * (n % 2) + GB, :, :]
-        else:
-            in1 = b_sb[:, b0 : b0 + GB, :, :]
+        m0 = 4 * (n % 2)
         nc.vector.tensor_tensor(
-            out=hp[n][:].rearrange("p (b k m t) -> p b k m t", b=GB, k=NO, m=NO),
-            in0=a_sb[:, b0 : b0 + GB, :, :].unsqueeze(2).to_broadcast(shape5),
-            in1=in1.unsqueeze(3).to_broadcast(shape5),
+            out=hp[n][:].rearrange("p (m r) -> p m r", m=4),
+            in0=a2[:, m0 : m0 + 4, :, :, :].rearrange("p m b d t -> p m (b d t)"),
+            in1=bk[:, n // 2, :, :, :].rearrange("p b d t -> p (b d t)").unsqueeze(1).to_broadcast([P, 4, 512]),
             op=ADD,
         )
 
-    def t1g(n):
-        if n not in G_GROUPS:
-            return
-        shape5 = [P, GPIECE, NO, NO, 4]
-        w = GPIECE * 256
-        for i in range(GB // GPIECE):
-            b0 = GB * n + GPIECE * i
-            piece = hp[n][:, w * i : w * i + w]
-            nc.gpsimd.tensor_tensor(
-                out=piece.rearrange("p (b k m t) -> p b k m t", b=GPIECE, k=NO, m=NO),
-                in0=a_sb[:, b0 : b0 + GPIECE, :, :].unsqueeze(2).to_broadcast(shape5),
-                in1=b_sb[:, b0 : b0 + GPIECE, :, :].unsqueeze(3).to_broadcast(shape5),
-                op=ADD,
-            )
-            nc.gpsimd.tensor_scalar(out=piece, in0=piece, scalar1=BIG, scalar2=0.0, op0=MIN, op1=MAX)
-
     def t2(n):
-        if not ok(n) or n in G_GROUPS:
-            return
-        nc.scalar.activation(out=hp[n][:], in_=hp[n][:], func=RELU)
+        if ok(n):
+            nc.scalar.activation(out=hp[n][:], in_=hp[n][:], func=RELU)
 
     def t3(n):
-        if not ok(n):
-            return
-        nc.vector.quantize_mx(out=hc[n][:].bitcast(FP8X4), scales=hs[n][:], in_=hp[n][:])
+        if ok(n):
+            nc.vector.quantize_mx(out=hc[n][:].bitcast(FP8X4), scales=hs[n][:], in_=hp[n][:])
 
     def l2(n, j):
         if not ok(n):
@@ -204,72 +179,69 @@ def body(tc, objs, W1, b1, W2, b2, out_0, out_1, const, ps, pres):
         )
 
     def t4(n, j):
-        if not ok(n):
-            return
-        nc.vector.tensor_tensor(out=xg[n][:, j, :], in0=zt[(n, j)][:], in1=b2bc[:], op=ADD)
+        if ok(n):
+            nc.vector.tensor_tensor(out=xg[n][:, j, :], in0=zt[(n, j)][:], in1=b2bc[:], op=ADD)
 
     def t5(n, j0, j1):
         if not ok(n):
             return
         nc.scalar.activation(out=xg[n][:, j0:j1, :], in_=xg[n][:, j0:j1, :], func=RELU)
-        nc.sync.dma_start(out=out0v[n][:, j0:j1, :], in_=xg[n][:, j0:j1, :])
+        nc.sync.dma_start(out=out0v[:, 4 * n + j0 : 4 * n + j1, :], in_=xg[n][:, j0:j1, :])
 
     def sm(n, j):
         if not ok(n):
             return
         tl = 4 * n + j
+        if tl == 0:
+            for c in range(4):
+                acc.append(pacc.tile([P, 512], F32, tag="acc", name="acc%d" % c))
         for c in range(4):
             nc.tensor.matmul(
-                out=st[:, SREG * c + 2 * tl : SREG * c + 2 * tl + SELW],
+                out=acc[c][:, 0:P],
                 lhsT=xg[n][:, j, P * c : P * c + P],
-                rhs=sel[:],
-                start=True,
-                stop=True,
+                rhs=ident[:],
+                is_transpose=True,
+                start=(tl == 0),
+                stop=(tl == NT - 1),
             )
 
-    layer1(0)
-    layer1(2)
-    t1g(4)
-    t1g(5)
+    for q in range(4):
+        layer1a(q)
+    for q in range(4):
+        layer1b(q)
     t1(0)
     flip(w2_sb, 0, 0, w2g[:], "s")
     flip(w2_sb, 0, 1, w2g[:], "s")
-    b2ps = ps.tile([P, 512], F32, tag="work")
+    b2ps = head_bank()
     nc.tensor.matmul(out=b2ps[:], lhsT=ones[:], rhs=bz[:], start=True, stop=True)
     b2bc = const.tile([P, G2], F32)
     nc.scalar.copy(out=b2bc[:], in_=b2ps[:])
     t2(0)
+    t1(1)
     quant(w2c, w2s, w2g, 0)
     quant(w2c, w2s, w2g, 1)
-    t1(1)
-    layer1(1)
-    layer1(3)
-    t1g(6)
-    t1g(7)
 
     last = NGRP - 1
     for i in range(-1, NGRP):
         t3(i + 1)
-        l2(i + 1, 0)
-        sm(i - 1, 2)
-        sm(i - 1, 3)
+        for j in range(4):
+            sm(i - 1, j)
         t2(i + 2)
         for j in range(4):
             t4(i, j)
-            if j < 3:
-                l2(i + 1, j + 1)
+            l2(i + 1, j)
             if i == last:
                 t5(i, j, j + 1)
                 sm(i, j)
             elif j % 2 == 1:
                 t5(i, j - 1, j + 1)
-        if i != last:
-            sm(i, 0)
-            sm(i, 1)
         t1(i + 3)
 
     sts = const.tile([P, 4, NB], F32)
-    nc.vector.tensor_copy(out=sts[:], in_=st[:, 0 : 4 * SREG].rearrange("p (c w) -> p c w", c=4)[:, :, 0:NB])
+    for c in range(4):
+        nc.vector.tensor_reduce(
+            out=sts[:, c, :], in_=acc[c][:, 0:P].rearrange("p (b d) -> p b d", d=2), axis=AXX, op=ADD
+        )
     fin = ps.tile([P, 512], F32, tag="work")
     for cp in range(2):
         nc.tensor.transpose(
@@ -283,8 +255,8 @@ def body(tc, objs, W1, b1, W2, b2, out_0, out_1, const, ps, pres):
 
 
 def tile_pairwiserelationmodule_pa_kernel(tc, objs, W1, b1, W2, b2, out_0, out_1):
-    with tc.tile_pool(name="const", bufs=1) as const, tc.psum_pool(name="ps", bufs=5) as ps, tc.psum_pool(
-        name="pres", bufs=1
-    ) as pres:
+    with tc.tile_pool(name="const", bufs=1) as const, tc.psum_pool(name="ps", bufs=4) as ps, tc.psum_pool(
+        name="pacc", bufs=4
+    ) as pacc:
         with tc.manual_schedule():
-            body(tc, objs, W1, b1, W2, b2, out_0, out_1, const, ps, pres)
+            body(tc, objs, W1, b1, W2, b2, out_0, out_1, const, ps, pacc)

@@ -9,6 +9,7 @@ FP8X4 = mybir.dt.float8_e4m3fn_x4
 ADD = mybir.AluOpType.add
 RELU = mybir.ActivationFunctionType.Relu
 AXX = mybir.AxisListType.X
+Z_GROUPS = (0, 1, 3, 4, 6)
 
 P = 128
 NB = 64
@@ -21,12 +22,12 @@ NGRP = 8
 NT = 32
 
 
-def body(tc, objs, W1, b1, W2, b2, out_0, out_1, const, ps, pacc):
+def body(tc, objs, W1, b1, W2, b2, out_0, out_1, const, ps, pacc, xtp):
     nc = tc.nc
     b1t = const.tile([P, 2, 2], BF16)
     nc.scalar.dma_start(out=b1t[:], in_=b1.rearrange("(u p e) -> p u e", u=2, e=2))
     bz = const.tile([P, G2], BF16)
-    nc.vector.memset(bz[:], 0.0)
+    nc.gpsimd.memset(bz[:], 0.0)
     nc.scalar.dma_start(out=bz[0:1, :], in_=b2.rearrange("(o n) -> o n", o=1))
     objs_sb = const.tile([P, 4, D], BF16)
     objv = objs.rearrange("b o d -> (b o) d").rearrange("(r p) d -> p r d", p=P)
@@ -42,14 +43,12 @@ def body(tc, objs, W1, b1, W2, b2, out_0, out_1, const, ps, pacc):
     ident = const.tile([P, P], F32)
     make_identity(nc, ident[:])
     ones = const.tile([P, P], BF16)
-    nc.vector.memset(ones[:], 1.0)
+    nc.gpsimd.memset(ones[:], 1.0)
 
     nbank = [0]
 
     def head_bank():
         nbank[0] += 1
-        if nbank[0] % 2 == 0:
-            return pacc.tile([P, 512], F32, tag="acc", name="hb")
         return ps.tile([P, 512], F32, tag="work", name="hw")
 
     def flip(src_sb, g, h, grouped, eng):
@@ -124,30 +123,44 @@ def body(tc, objs, W1, b1, W2, b2, out_0, out_1, const, ps, pacc):
         nc.vector.tensor_tensor(
             out=a2[:, :, bs, 0, :], in0=bank[:].rearrange("p (t b m) -> p m b t", t=4, b=16), in1=b1b, op=ADD
         )
-        nc.scalar.copy(out=a2[:, :, bs, 1, :], in_=a2[:, :, bs, 0, :])
 
     def layer1b(q):
         bank = mx1(1, q)
         bs = slice(16 * q, 16 * q + 16)
-        src = bank[:].rearrange("p (t b kh kl) -> p kh kl b t", t=4, b=16, kh=2)
-        for kh in range(2):
-            nc.scalar.copy(out=bk[:, :, bs, kh, :], in_=src[:, kh])
+        nc.scalar.copy(
+            out=bk[:, :, bs, :, :].rearrange("p l b h t -> p l (b h) t"),
+            in_=bank[:].rearrange("p (t i l) -> p l i t", t=4, l=4),
+        )
 
     hp = [const.tile([P, 2048], BF16, align_bytes=64, name="hp%d" % n) for n in range(NGRP)]
     hc = [const.tile([P, 512], U32, align_bytes=64, name="hc%d" % n) for n in range(NGRP)]
     hs = [const.tile([P, 512], U8, align_bytes=64, name="hs%d" % n) for n in range(NGRP)]
     xg = [const.tile([P, 4, G2], F32, name="xg%d" % n) for n in range(NGRP)]
     zt = {}
+    xts = {}
     acc = []
     out0v = out_0.rearrange("b q g -> (b q) g").rearrange("(p t) g -> p t g", t=NT)
 
     def ok(n):
         return 0 <= n < NGRP
 
+    def dup():
+        for h in range(2):
+            nc.scalar.copy(out=a2[:, 4 * h : 4 * h + 4, :, 1, :], in_=a2[:, 4 * h : 4 * h + 4, :, 0, :])
+
     def t1(n):
         if not ok(n):
             return
         m0 = 4 * (n % 2)
+        if n < 2:
+            for j in range(4):
+                nc.vector.tensor_tensor(
+                    out=hp[n][:, 512 * j : 512 * j + 512].rearrange("p (b d t) -> p b d t", d=2, t=4),
+                    in0=a2[:, m0 + j, :, 0, :].unsqueeze(2).to_broadcast([P, NB, 2, 4]),
+                    in1=bk[:, n // 2, :, :, :],
+                    op=ADD,
+                )
+            return
         nc.vector.tensor_tensor(
             out=hp[n][:].rearrange("p (m r) -> p m r", m=4),
             in0=a2[:, m0 : m0 + 4, :, :, :].rearrange("p m b d t -> p m (b d t)"),
@@ -157,7 +170,7 @@ def body(tc, objs, W1, b1, W2, b2, out_0, out_1, const, ps, pacc):
 
     def t2(n):
         if ok(n):
-            nc.scalar.activation(out=hp[n][:], in_=hp[n][:], func=RELU)
+            nc.vector.tensor_scalar_max(out=hp[n][:], in0=hp[n][:], scalar1=0.0)
 
     def t3(n):
         if ok(n):
@@ -168,15 +181,43 @@ def body(tc, objs, W1, b1, W2, b2, out_0, out_1, const, ps, pacc):
             return
         z = ps.tile([P, 512], F32, tag="work", name="z")
         zt[(n, j)] = z
-        nc.tensor.matmul_mx(
-            out=z[:],
-            lhsT=hc[n][:, P * j : P * j + P].bitcast(FP8X4),
-            lhsT_scale=hs[n][:, P * j : P * j + P],
-            rhs=w2c[:].bitcast(FP8X4),
-            rhs_scale=w2s[:],
-            start=True,
-            stop=True,
-        )
+        cols = slice(P * j, P * j + P)
+        if n in Z_GROUPS:
+            nc.tensor.matmul_mx(
+                out=z[:],
+                lhsT=w2c[:, cols].bitcast(FP8X4),
+                lhsT_scale=w2s[:, cols],
+                rhs=hc[n][:].bitcast(FP8X4),
+                rhs_scale=hs[n][:],
+                start=True,
+                stop=True,
+            )
+        else:
+            nc.tensor.matmul_mx(
+                out=z[:],
+                lhsT=hc[n][:, cols].bitcast(FP8X4),
+                lhsT_scale=hs[n][:, cols],
+                rhs=w2c[:].bitcast(FP8X4),
+                rhs_scale=w2s[:],
+                start=True,
+                stop=True,
+            )
+
+    def t4z(n, c):
+        if c == 0:
+            xts[n] = xtp.tile([P, 4, 512], F32, name="xt")
+        nc.scalar.activation(out=xts[n][:, c, :], in_=zt[(n, c)][:], func=RELU, bias=b2t[:, c : c + 1])
+
+    def btr(n, j):
+        xb = ps.tile([P, 512], F32, tag="work", name="xb")
+        zt[(n, 4 + j)] = xb
+        for c in range(4):
+            nc.tensor.transpose(xb[:, P * c : P * c + P], xts[n][:, c, P * j : P * j + P], ident[:])
+
+    def ex(n, j):
+        nc.scalar.copy(out=xg[n][:, j, :], in_=zt[(n, 4 + j)][:])
+        if j % 2 == 1:
+            nc.sync.dma_start(out=out0v[:, 4 * n + j - 1 : 4 * n + j + 1, :], in_=xg[n][:, j - 1 : j + 1, :])
 
     def t4(n, j):
         if ok(n):
@@ -193,16 +234,15 @@ def body(tc, objs, W1, b1, W2, b2, out_0, out_1, const, ps, pacc):
             return
         tl = 4 * n + j
         if tl == 0:
-            for c in range(4):
-                acc.append(pacc.tile([P, 512], F32, tag="acc", name="acc%d" % c))
+            acc.append(pacc.tile([P, 512], F32, name="acc"))
         for c in range(4):
             nc.tensor.matmul(
-                out=acc[c][:, 0:P],
+                out=acc[0][:, P * c : P * c + P],
                 lhsT=xg[n][:, j, P * c : P * c + P],
                 rhs=ident[:],
                 is_transpose=True,
-                start=(tl == 0),
-                stop=(tl == NT - 1),
+                start=(tl == 0 and c == 0),
+                stop=(tl == NT - 1 and c == 3),
             )
 
     for q in range(4):
@@ -216,32 +256,61 @@ def body(tc, objs, W1, b1, W2, b2, out_0, out_1, const, ps, pacc):
     nc.tensor.matmul(out=b2ps[:], lhsT=ones[:], rhs=bz[:], start=True, stop=True)
     b2bc = const.tile([P, G2], F32)
     nc.scalar.copy(out=b2bc[:], in_=b2ps[:])
+    b2tp = head_bank()
+    for c in range(4):
+        nc.tensor.transpose(b2tp[:, P * c : P * c + P], b2bc[:, P * c : P * c + P], ident[:])
+    b2t = const.tile([P, 4], F32)
+    nc.scalar.copy(out=b2t[:], in_=b2tp[:].rearrange("p (c w) -> p c w", c=4)[:, :, 0])
+    dup()
     t2(0)
-    t1(1)
     quant(w2c, w2s, w2g, 0)
     quant(w2c, w2s, w2g, 1)
+    t3(0)
+    for j in range(4):
+        l2(0, j)
+    t1(1)
+    t2(1)
+    t3(1)
 
     last = NGRP - 1
-    for i in range(-1, NGRP):
-        t3(i + 1)
-        for j in range(4):
-            sm(i - 1, j)
-        t2(i + 2)
-        for j in range(4):
-            t4(i, j)
-            l2(i + 1, j)
-            if i == last:
-                t5(i, j, j + 1)
+    for i in range(NGRP):
+        if i in Z_GROUPS:
+            for c in range(4):
+                t4z(i, c)
+            for j in range(4):
+                l2(i + 1, j)
+            t1(i + 2)
+            for j in range(3):
+                btr(i, j)
+            ex(i, 0)
+            btr(i, 3)
+            t2(i + 2)
+            for j in range(1, 4):
+                ex(i, j)
+            for j in range(4):
                 sm(i, j)
-            elif j % 2 == 1:
-                t5(i, j - 1, j + 1)
-        t1(i + 3)
+            t3(i + 2)
+        else:
+            for j in range(4):
+                t4(i, j)
+                if i == last:
+                    t5(i, j, j + 1)
+                    sm(i, j)
+                elif j % 2 == 1:
+                    t5(i, j - 1, j + 1)
+            for j in range(4):
+                l2(i + 1, j)
+            t1(i + 2)
+            if i != last:
+                for j in range(4):
+                    sm(i, j)
+            t2(i + 2)
+            t3(i + 2)
 
     sts = const.tile([P, 4, NB], F32)
-    for c in range(4):
-        nc.vector.tensor_reduce(
-            out=sts[:, c, :], in_=acc[c][:, 0:P].rearrange("p (b d) -> p b d", d=2), axis=AXX, op=ADD
-        )
+    nc.vector.tensor_reduce(
+        out=sts[:].rearrange("p c b -> p (c b)"), in_=acc[0][:].rearrange("p (i d) -> p i d", d=2), axis=AXX, op=ADD
+    )
     fin = ps.tile([P, 512], F32, tag="work")
     for cp in range(2):
         nc.tensor.transpose(
@@ -255,8 +324,8 @@ def body(tc, objs, W1, b1, W2, b2, out_0, out_1, const, ps, pacc):
 
 
 def tile_pairwiserelationmodule_pa_kernel(tc, objs, W1, b1, W2, b2, out_0, out_1):
-    with tc.tile_pool(name="const", bufs=1) as const, tc.psum_pool(name="ps", bufs=4) as ps, tc.psum_pool(
-        name="pacc", bufs=4
-    ) as pacc:
+    with tc.tile_pool(name="const", bufs=1) as const, tc.tile_pool(name="xtp", bufs=2) as xtp, tc.psum_pool(
+        name="ps", bufs=7
+    ) as ps, tc.psum_pool(name="pacc", bufs=1) as pacc:
         with tc.manual_schedule():
-            body(tc, objs, W1, b1, W2, b2, out_0, out_1, const, ps, pacc)
+            body(tc, objs, W1, b1, W2, b2, out_0, out_1, const, ps, pacc, xtp)

@@ -8,324 +8,236 @@ U8 = mybir.dt.uint8
 FP8X4 = mybir.dt.float8_e4m3fn_x4
 ADD = mybir.AluOpType.add
 RELU = mybir.ActivationFunctionType.Relu
-AXX = mybir.AxisListType.X
-Z_GROUPS = (0, 1, 3, 4, 6)
 
 P = 128
-NB = 64
-NO = 8
-D = 512
-G1 = 512
-G2 = 512
-FLOPS = 2 * NB * NO * NO * (2 * D) * G1 + 2 * NB * NO * NO * G1 * G2
-NGRP = 8
-NT = 32
-
-
-def body(tc, objs, W1, b1, W2, b2, out_0, out_1, const, ps, pacc, xtp):
-    nc = tc.nc
-    b1t = const.tile([P, 2, 2], BF16)
-    nc.scalar.dma_start(out=b1t[:], in_=b1.rearrange("(u p e) -> p u e", u=2, e=2))
-    bz = const.tile([P, G2], BF16)
-    nc.gpsimd.memset(bz[:], 0.0)
-    nc.scalar.dma_start(out=bz[0:1, :], in_=b2.rearrange("(o n) -> o n", o=1))
-    objs_sb = const.tile([P, 4, D], BF16)
-    objv = objs.rearrange("b o d -> (b o) d").rearrange("(r p) d -> p r d", p=P)
-    w1_sb = const.tile([P, 4, 2 * D], BF16)
-    w1v = W1.rearrange("(u p e) c -> u p e c", u=2, e=2)
-    nc.sync.dma_start(out=objs_sb[:], in_=objv)
-    for g in range(2):
-        for u in range(2):
-            nc.sync.dma_start(out=w1_sb[:, 2 * u : 2 * u + 2, D * g : D * g + D], in_=w1v[u][:, :, D * g : D * g + D])
-    w2_sb = const.tile([P, 4, G1], BF16)
-    nc.sync.dma_start(out=w2_sb[:], in_=W2.rearrange("(j p) c -> p j c", p=P))
-
-    ident = const.tile([P, P], F32)
-    make_identity(nc, ident[:])
-    ones = const.tile([P, P], BF16)
-    nc.gpsimd.memset(ones[:], 1.0)
-
-    nbank = [0]
-
-    def head_bank():
-        nbank[0] += 1
-        return ps.tile([P, 512], F32, tag="work", name="hw")
-
-    def flip(src_sb, g, h, grouped, eng):
-        gw = grouped.bitcast(F32).rearrange("p (c u) -> p c u", u=2)
-        bank = head_bank()
-        for rt in range(2):
-            words = src_sb[:, 2 * h + rt, :].bitcast(F32)
-            for u in range(2):
-                nc.tensor.transpose(
-                    bank[:, (2 * rt + u) * P : (2 * rt + u + 1) * P],
-                    words[:, 256 * g + P * u : 256 * g + P * u + P],
-                    ident[:],
-                )
-        dst = gw[:, 256 * h : 256 * h + 256, :].rearrange("p (rt c) u -> p rt c u", rt=2)
-        src = bank[:].rearrange("p (rt u c) -> p rt c u", rt=2, u=2)
-        if eng == "s":
-            nc.scalar.copy(out=dst, in_=src)
-        else:
-            nc.vector.tensor_copy(out=dst, in_=src)
-
-    def quant(codes, scales, grouped, h):
-        nc.vector.quantize_mx(
-            out=codes[:, 256 * h : 256 * h + 256].bitcast(FP8X4),
-            scales=scales[:, 256 * h : 256 * h + 256],
-            in_=grouped[:, 1024 * h : 1024 * h + 1024],
-        )
-
-    og = const.tile([P, 2048], BF16, align_bytes=64)
-    oc = const.tile([P, 512], U32, align_bytes=64)
-    osc = const.tile([P, 512], U8, align_bytes=64)
-    w1g = [const.tile([P, 2048], BF16, align_bytes=64, name="w1g%d" % g) for g in range(2)]
-    w1c = [const.tile([P, 512], U32, align_bytes=64, name="w1c%d" % g) for g in range(2)]
-    w1s = [const.tile([P, 512], U8, align_bytes=64, name="w1s%d" % g) for g in range(2)]
-    w2g = const.tile([P, 2048], BF16, align_bytes=64)
-    w2c = const.tile([P, 512], U32, align_bytes=64)
-    w2s = const.tile([P, 512], U8, align_bytes=64)
-
-    flip(objs_sb, 0, 0, og[:], "s")
-    flip(objs_sb, 0, 1, og[:], "v")
-    flip(w1_sb, 0, 0, w1g[0][:], "s")
-    quant(oc, osc, og, 0)
-    flip(w1_sb, 0, 1, w1g[0][:], "v")
-    quant(oc, osc, og, 1)
-    quant(w1c[0], w1s[0], w1g[0], 0)
-    quant(w1c[0], w1s[0], w1g[0], 1)
-    flip(w1_sb, 1, 0, w1g[1][:], "s")
-    flip(w1_sb, 1, 1, w1g[1][:], "v")
-    quant(w1c[1], w1s[1], w1g[1], 0)
-    quant(w1c[1], w1s[1], w1g[1], 1)
-
-    a2 = const.tile([P, NO, NB, 2, 4], F32)
-    bk = const.tile([P, 4, NB, 2, 4], F32)
-    b1b = b1t[:].rearrange("p u e -> p (u e)").unsqueeze(1).unsqueeze(1).to_broadcast([P, NO, 16, 4])
-
-    def mx1(g, q):
-        bank = head_bank()
-        for t in range(4):
-            nc.tensor.matmul_mx(
-                out=bank[:, P * t : P * t + P],
-                lhsT=w1c[g][:, P * t : P * t + P].bitcast(FP8X4),
-                lhsT_scale=w1s[g][:, P * t : P * t + P],
-                rhs=oc[:, P * q : P * q + P].bitcast(FP8X4),
-                rhs_scale=osc[:, P * q : P * q + P],
-                start=True,
-                stop=True,
-            )
-        return bank
-
-    def layer1a(q):
-        bank = mx1(0, q)
-        bs = slice(16 * q, 16 * q + 16)
-        nc.vector.tensor_tensor(
-            out=a2[:, :, bs, 0, :], in0=bank[:].rearrange("p (t b m) -> p m b t", t=4, b=16), in1=b1b, op=ADD
-        )
-
-    def layer1b(q):
-        bank = mx1(1, q)
-        bs = slice(16 * q, 16 * q + 16)
-        nc.scalar.copy(
-            out=bk[:, :, bs, :, :].rearrange("p l b h t -> p l (b h) t"),
-            in_=bank[:].rearrange("p (t i l) -> p l i t", t=4, l=4),
-        )
-
-    hp = [const.tile([P, 2048], BF16, align_bytes=64, name="hp%d" % n) for n in range(NGRP)]
-    hc = [const.tile([P, 512], U32, align_bytes=64, name="hc%d" % n) for n in range(NGRP)]
-    hs = [const.tile([P, 512], U8, align_bytes=64, name="hs%d" % n) for n in range(NGRP)]
-    xg = [const.tile([P, 4, G2], F32, name="xg%d" % n) for n in range(NGRP)]
-    zt = {}
-    xts = {}
-    acc = []
-    out0v = out_0.rearrange("b q g -> (b q) g").rearrange("(p t) g -> p t g", t=NT)
-
-    def ok(n):
-        return 0 <= n < NGRP
-
-    def dup():
-        for h in range(2):
-            nc.scalar.copy(out=a2[:, 4 * h : 4 * h + 4, :, 1, :], in_=a2[:, 4 * h : 4 * h + 4, :, 0, :])
-
-    def t1(n):
-        if not ok(n):
-            return
-        m0 = 4 * (n % 2)
-        if n < 2:
-            for j in range(4):
-                nc.vector.tensor_tensor(
-                    out=hp[n][:, 512 * j : 512 * j + 512].rearrange("p (b d t) -> p b d t", d=2, t=4),
-                    in0=a2[:, m0 + j, :, 0, :].unsqueeze(2).to_broadcast([P, NB, 2, 4]),
-                    in1=bk[:, n // 2, :, :, :],
-                    op=ADD,
-                )
-            return
-        nc.vector.tensor_tensor(
-            out=hp[n][:].rearrange("p (m r) -> p m r", m=4),
-            in0=a2[:, m0 : m0 + 4, :, :, :].rearrange("p m b d t -> p m (b d t)"),
-            in1=bk[:, n // 2, :, :, :].rearrange("p b d t -> p (b d t)").unsqueeze(1).to_broadcast([P, 4, 512]),
-            op=ADD,
-        )
-
-    def t2(n):
-        if ok(n):
-            nc.vector.tensor_scalar_max(out=hp[n][:], in0=hp[n][:], scalar1=0.0)
-
-    def t3(n):
-        if ok(n):
-            nc.vector.quantize_mx(out=hc[n][:].bitcast(FP8X4), scales=hs[n][:], in_=hp[n][:])
-
-    def l2(n, j):
-        if not ok(n):
-            return
-        z = ps.tile([P, 512], F32, tag="work", name="z")
-        zt[(n, j)] = z
-        cols = slice(P * j, P * j + P)
-        if n in Z_GROUPS:
-            nc.tensor.matmul_mx(
-                out=z[:],
-                lhsT=w2c[:, cols].bitcast(FP8X4),
-                lhsT_scale=w2s[:, cols],
-                rhs=hc[n][:].bitcast(FP8X4),
-                rhs_scale=hs[n][:],
-                start=True,
-                stop=True,
-            )
-        else:
-            nc.tensor.matmul_mx(
-                out=z[:],
-                lhsT=hc[n][:, cols].bitcast(FP8X4),
-                lhsT_scale=hs[n][:, cols],
-                rhs=w2c[:].bitcast(FP8X4),
-                rhs_scale=w2s[:],
-                start=True,
-                stop=True,
-            )
-
-    def t4z(n, c):
-        if c == 0:
-            xts[n] = xtp.tile([P, 4, 512], F32, name="xt")
-        nc.scalar.activation(out=xts[n][:, c, :], in_=zt[(n, c)][:], func=RELU, bias=b2t[:, c : c + 1])
-
-    def btr(n, j):
-        xb = ps.tile([P, 512], F32, tag="work", name="xb")
-        zt[(n, 4 + j)] = xb
-        for c in range(4):
-            nc.tensor.transpose(xb[:, P * c : P * c + P], xts[n][:, c, P * j : P * j + P], ident[:])
-
-    def ex(n, j):
-        nc.scalar.copy(out=xg[n][:, j, :], in_=zt[(n, 4 + j)][:])
-        if j % 2 == 1:
-            nc.sync.dma_start(out=out0v[:, 4 * n + j - 1 : 4 * n + j + 1, :], in_=xg[n][:, j - 1 : j + 1, :])
-
-    def t4(n, j):
-        if ok(n):
-            nc.vector.tensor_tensor(out=xg[n][:, j, :], in0=zt[(n, j)][:], in1=b2bc[:], op=ADD)
-
-    def t5(n, j0, j1):
-        if not ok(n):
-            return
-        nc.scalar.activation(out=xg[n][:, j0:j1, :], in_=xg[n][:, j0:j1, :], func=RELU)
-        nc.sync.dma_start(out=out0v[:, 4 * n + j0 : 4 * n + j1, :], in_=xg[n][:, j0:j1, :])
-
-    def sm(n, j):
-        if not ok(n):
-            return
-        tl = 4 * n + j
-        if tl == 0:
-            acc.append(pacc.tile([P, 512], F32, name="acc"))
-        for c in range(4):
-            nc.tensor.matmul(
-                out=acc[0][:, P * c : P * c + P],
-                lhsT=xg[n][:, j, P * c : P * c + P],
-                rhs=ident[:],
-                is_transpose=True,
-                start=(tl == 0 and c == 0),
-                stop=(tl == NT - 1 and c == 3),
-            )
-
-    for q in range(4):
-        layer1a(q)
-    for q in range(4):
-        layer1b(q)
-    t1(0)
-    flip(w2_sb, 0, 0, w2g[:], "s")
-    flip(w2_sb, 0, 1, w2g[:], "s")
-    b2ps = head_bank()
-    nc.tensor.matmul(out=b2ps[:], lhsT=ones[:], rhs=bz[:], start=True, stop=True)
-    b2bc = const.tile([P, G2], F32)
-    nc.scalar.copy(out=b2bc[:], in_=b2ps[:])
-    b2tp = head_bank()
-    for c in range(4):
-        nc.tensor.transpose(b2tp[:, P * c : P * c + P], b2bc[:, P * c : P * c + P], ident[:])
-    b2t = const.tile([P, 4], F32)
-    nc.scalar.copy(out=b2t[:], in_=b2tp[:].rearrange("p (c w) -> p c w", c=4)[:, :, 0])
-    dup()
-    t2(0)
-    quant(w2c, w2s, w2g, 0)
-    quant(w2c, w2s, w2g, 1)
-    t3(0)
-    for j in range(4):
-        l2(0, j)
-    t1(1)
-    t2(1)
-    t3(1)
-
-    last = NGRP - 1
-    for i in range(NGRP):
-        if i in Z_GROUPS:
-            for c in range(4):
-                t4z(i, c)
-            for j in range(4):
-                l2(i + 1, j)
-            t1(i + 2)
-            for j in range(3):
-                btr(i, j)
-            ex(i, 0)
-            btr(i, 3)
-            t2(i + 2)
-            for j in range(1, 4):
-                ex(i, j)
-            for j in range(4):
-                sm(i, j)
-            t3(i + 2)
-        else:
-            for j in range(4):
-                t4(i, j)
-                if i == last:
-                    t5(i, j, j + 1)
-                    sm(i, j)
-                elif j % 2 == 1:
-                    t5(i, j - 1, j + 1)
-            for j in range(4):
-                l2(i + 1, j)
-            t1(i + 2)
-            if i != last:
-                for j in range(4):
-                    sm(i, j)
-            t2(i + 2)
-            t3(i + 2)
-
-    sts = const.tile([P, 4, NB], F32)
-    nc.vector.tensor_reduce(
-        out=sts[:].rearrange("p c b -> p (c b)"), in_=acc[0][:].rearrange("p (i d) -> p i d", d=2), axis=AXX, op=ADD
-    )
-    fin = ps.tile([P, 512], F32, tag="work")
-    for cp in range(2):
-        nc.tensor.transpose(
-            fin[:, P * cp : P * cp + P], sts[:, 2 * cp : 2 * cp + 2, :].rearrange("p a b -> p (a b)"), ident[:]
-        )
-    s_sb = const.tile([P, 2, P], F32)
-    nc.vector.tensor_copy(out=s_sb[:].rearrange("p a g -> p (a g)"), in_=fin[:, 0 : 2 * P])
-    out1v = out_1.rearrange("b (cp cc g) -> cc b cp g", cp=2, cc=2)
-    for cc in range(2):
-        nc.sync.dma_start(out=out1v[cc], in_=s_sb[64 * cc : 64 * cc + 64, :, :])
+SETS = 64
+OBJECTS = 8
+WIDTH = 512
+PACK = 4
+TILES = 32
+GROUP = 4
+GROUPS = TILES // GROUP
+WORK_BANKS = 7
+FLOPS = 2 * SETS * OBJECTS * OBJECTS * (2 * WIDTH * WIDTH + WIDTH * WIDTH)
 
 
 def tile_pairwiserelationmodule_pa_kernel(tc, objs, W1, b1, W2, b2, out_0, out_1):
-    with tc.tile_pool(name="const", bufs=1) as const, tc.tile_pool(name="xtp", bufs=2) as xtp, tc.psum_pool(
-        name="ps", bufs=7
-    ) as ps, tc.psum_pool(name="pacc", bufs=1) as pacc:
-        with tc.manual_schedule():
-            body(tc, objs, W1, b1, W2, b2, out_0, out_1, const, ps, pacc, xtp)
+    nc = tc.nc
+    with tc.tile_pool(name="sbuf", bufs=1) as sbuf, tc.psum_pool(name="work", bufs=WORK_BANKS) as work, tc.psum_pool(
+        name="sums", bufs=1
+    ) as sums, tc.manual_schedule():
+
+        def bank():
+            return work.tile([P, WIDTH], F32, tag="bank", name="bank")
+
+        b1_pt = sbuf.tile([P, 2, 2], BF16)
+        nc.scalar.dma_start(out=b1_pt[:], in_=b1.rearrange("(u p e) -> p u e", u=2, e=2))
+        b2_row = sbuf.tile([P, WIDTH], BF16)
+        nc.gpsimd.memset(b2_row[:], 0.0)
+        nc.scalar.dma_start(out=b2_row[0:1, :], in_=b2.rearrange("(o n) -> o n", o=1))
+        objs_sb = sbuf.tile([P, 4, WIDTH], BF16)
+        nc.sync.dma_start(out=objs_sb[:], in_=objs.rearrange("b o d -> (b o) d").rearrange("(p l) d -> p l d", l=4))
+        w1_sb = sbuf.tile([P, 4, 2 * WIDTH], BF16)
+        w1_rows = W1.rearrange("(u p e) c -> u p e c", u=2, e=2)
+        for half in range(2):
+            cols = slice(WIDTH * half, WIDTH * half + WIDTH)
+            for u in range(2):
+                nc.sync.dma_start(out=w1_sb[:, 2 * u : 2 * u + 2, cols], in_=w1_rows[u][:, :, cols])
+        w2_sb = sbuf.tile([P, 4, WIDTH], BF16)
+        nc.sync.dma_start(out=w2_sb[:], in_=W2.rearrange("(j p) c -> p j c", p=P))
+
+        identity = sbuf.tile([P, P], F32)
+        make_identity(nc, identity[:])
+        ones = sbuf.tile([P, P], BF16)
+        nc.gpsimd.memset(ones[:], 1.0)
+
+        def operand(name):
+            return (
+                sbuf.tile([P, PACK * WIDTH], BF16, align_bytes=64, name=name + "_bf"),
+                sbuf.tile([P, WIDTH], U32, align_bytes=64, name=name + "_words"),
+                sbuf.tile([P, WIDTH], U8, align_bytes=64, name=name + "_scales"),
+            )
+
+        def transpose_half(rows_sb, first_word, side, dst, copy):
+            planes = bank()
+            for slot in range(2):
+                words = rows_sb[:, 2 * side + slot, :].bitcast(F32)
+                for u in range(2):
+                    nc.tensor.transpose(
+                        planes[:, (2 * slot + u) * P : (2 * slot + u + 1) * P],
+                        words[:, first_word + P * u : first_word + P * u + P],
+                        identity[:],
+                    )
+            copy(
+                out=dst[0][:, 1024 * side : 1024 * side + 1024].bitcast(F32).rearrange("p (s c u) -> p s c u", s=2, u=2),
+                in_=planes[:].rearrange("p (s u c) -> p s c u", s=2, u=2),
+            )
+
+        def quantise_half(dst, side):
+            nc.vector.quantize_mx(
+                out=dst[1][:, 256 * side : 256 * side + 256].bitcast(FP8X4),
+                scales=dst[2][:, 256 * side : 256 * side + 256],
+                in_=dst[0][:, 1024 * side : 1024 * side + 1024],
+            )
+
+        objs_q = operand("objs")
+        w1_q = [operand("w1a"), operand("w1b")]
+        w2_q = operand("w2")
+
+        transpose_half(objs_sb, 0, 0, objs_q, nc.scalar.copy)
+        transpose_half(objs_sb, 0, 1, objs_q, nc.vector.tensor_copy)
+        transpose_half(w1_sb, 0, 0, w1_q[0], nc.scalar.copy)
+        quantise_half(objs_q, 0)
+        transpose_half(w1_sb, 0, 1, w1_q[0], nc.vector.tensor_copy)
+        quantise_half(objs_q, 1)
+        quantise_half(w1_q[0], 0)
+        quantise_half(w1_q[0], 1)
+        transpose_half(w1_sb, 256, 0, w1_q[1], nc.scalar.copy)
+        transpose_half(w1_sb, 256, 1, w1_q[1], nc.vector.tensor_copy)
+        quantise_half(w1_q[1], 0)
+        quantise_half(w1_q[1], 1)
+
+        a_sb = sbuf.tile([P, OBJECTS, SETS, PACK], F32)
+        b_sb = sbuf.tile([P, 4, SETS, 2, PACK], F32)
+        b1_spread = b1_pt[:].rearrange("p u e -> p (u e)").unsqueeze(1).unsqueeze(1).to_broadcast([P, 2, SETS, PACK])
+
+        def first_layer(half, kl):
+            acc = bank()
+            for t in range(PACK):
+                nc.tensor.matmul_mx(
+                    out=acc[:, P * t : P * t + P],
+                    lhsT=w1_q[half][1][:, P * t : P * t + P].bitcast(FP8X4),
+                    lhsT_scale=w1_q[half][2][:, P * t : P * t + P],
+                    rhs=objs_q[1][:, P * kl : P * kl + P].bitcast(FP8X4),
+                    rhs_scale=objs_q[2][:, P * kl : P * kl + P],
+                    start=True,
+                    stop=True,
+                )
+            if half == 0:
+                nc.vector.tensor_tensor(
+                    out=a_sb[:, kl : OBJECTS : 4, :, :],
+                    in0=acc[:].rearrange("p (t b h) -> p h b t", t=PACK, h=2),
+                    in1=b1_spread,
+                    op=ADD,
+                )
+            else:
+                nc.scalar.copy(
+                    out=b_sb[:, kl, :, :, :].rearrange("p b h t -> p (b h) t"),
+                    in_=acc[:].rearrange("p (t i) -> p i t", t=PACK),
+                )
+
+        h_bf = [sbuf.tile([P, PACK * WIDTH], BF16, align_bytes=64, name="h_bf%d" % g) for g in range(GROUPS)]
+        h_words = [sbuf.tile([P, WIDTH], U32, align_bytes=64, name="h_words%d" % g) for g in range(GROUPS)]
+        h_scales = [sbuf.tile([P, WIDTH], U8, align_bytes=64, name="h_scales%d" % g) for g in range(GROUPS)]
+        x_sb = [sbuf.tile([P, GROUP, WIDTH], F32, name="x_sb%d" % g) for g in range(GROUPS)]
+        z_banks = {}
+        sum_bank = sums.tile([P, WIDTH], F32)
+        out_rows = out_0.rearrange("b q n -> (b q) n").rearrange("(p t) n -> p t n", t=TILES)
+
+        def exists(g):
+            return 0 <= g < GROUPS
+
+        def add_a_b(g):
+            if not exists(g):
+                return
+            for j in range(GROUP):
+                nc.vector.tensor_tensor(
+                    out=h_bf[g][:, WIDTH * j : WIDTH * j + WIDTH].rearrange("p (b h t) -> p b h t", h=2, t=PACK),
+                    in0=a_sb[:, (GROUP * g + j) % OBJECTS, :, :].unsqueeze(2).to_broadcast([P, SETS, 2, PACK]),
+                    in1=b_sb[:, g // 2, :, :, :],
+                    op=ADD,
+                )
+
+        def relu_h(g):
+            if exists(g):
+                nc.scalar.activation(out=h_bf[g][:], in_=h_bf[g][:], func=RELU)
+
+        def quantise_h(g):
+            if exists(g):
+                nc.vector.quantize_mx(out=h_words[g][:].bitcast(FP8X4), scales=h_scales[g][:], in_=h_bf[g][:])
+
+        def second_layer(g, j):
+            if not exists(g):
+                return
+            z_banks[(g, j)] = bank()
+            nc.tensor.matmul_mx(
+                out=z_banks[(g, j)][:],
+                lhsT=h_words[g][:, P * j : P * j + P].bitcast(FP8X4),
+                lhsT_scale=h_scales[g][:, P * j : P * j + P],
+                rhs=w2_q[1][:].bitcast(FP8X4),
+                rhs_scale=w2_q[2][:],
+                start=True,
+                stop=True,
+            )
+
+        def add_b2(g, j):
+            if exists(g):
+                nc.vector.tensor_tensor(out=x_sb[g][:, j, :], in0=z_banks[(g, j)][:], in1=b2_spread[:], op=ADD)
+
+        def relu_store_sum(g, first, stop):
+            if not exists(g):
+                return
+            nc.scalar.activation(out=x_sb[g][:, first:stop, :], in_=x_sb[g][:, first:stop, :], func=RELU)
+            nc.sync.dma_start(out=out_rows[:, GROUP * g + first : GROUP * g + stop, :], in_=x_sb[g][:, first:stop, :])
+            for j in range(first, stop):
+                for c in range(4):
+                    nc.tensor.matmul(
+                        out=sum_bank[:, P * c : P * c + P],
+                        lhsT=x_sb[g][:, j, P * c : P * c + P],
+                        rhs=identity[:],
+                        is_transpose=True,
+                        start=(g == 0 and j == 0 and c == 0),
+                        stop=(g == GROUPS - 1 and j == GROUP - 1 and c == 3),
+                    )
+
+        for kl in range(4):
+            first_layer(0, kl)
+        first_layer(1, 0)
+        add_a_b(0)
+        transpose_half(w2_sb, 0, 0, w2_q, nc.scalar.copy)
+        transpose_half(w2_sb, 0, 1, w2_q, nc.scalar.copy)
+        b2_bank = bank()
+        nc.tensor.matmul(out=b2_bank[:], lhsT=ones[:], rhs=b2_row[:], start=True, stop=True)
+        b2_spread = sbuf.tile([P, WIDTH], F32)
+        nc.scalar.copy(out=b2_spread[:], in_=b2_bank[:])
+        for kl in range(1, 4):
+            first_layer(1, kl)
+        relu_h(0)
+        add_a_b(1)
+        quantise_half(w2_q, 0)
+        quantise_half(w2_q, 1)
+
+        for i in range(-1, GROUPS):
+            quantise_h(i + 1)
+            for j in range(WORK_BANKS - GROUP):
+                second_layer(i + 1, j)
+            relu_h(i + 2)
+            for j in range(GROUP):
+                add_b2(i, j)
+                if j == 0:
+                    second_layer(i + 1, GROUP - 1)
+                if i == GROUPS - 1:
+                    relu_store_sum(i, j, j + 1)
+                elif j % 2 == 1:
+                    relu_store_sum(i, j - 1, j + 1)
+            add_a_b(i + 3)
+
+        s_t = sbuf.tile([P, 4, SETS], F32)
+        nc.vector.tensor_reduce(
+            out=s_t[:].rearrange("p c b -> p (c b)"),
+            in_=sum_bank[:].rearrange("p (i h) -> p i h", h=2),
+            axis=mybir.AxisListType.X,
+            op=ADD,
+        )
+        s_bank = bank()
+        for pair in range(2):
+            nc.tensor.transpose(
+                s_bank[:, P * pair : P * pair + P],
+                s_t[:, 2 * pair : 2 * pair + 2, :].rearrange("p c b -> p (c b)"),
+                identity[:],
+            )
+        s_sb = sbuf.tile([P, 2, P], F32)
+        nc.vector.tensor_copy(out=s_sb[:].rearrange("p a n -> p (a n)"), in_=s_bank[:, 0 : 2 * P])
+        s_rows = out_1.rearrange("b (pair odd n) -> odd b pair n", pair=2, odd=2)
+        for odd in range(2):
+            nc.sync.dma_start(out=s_rows[odd], in_=s_sb[SETS * odd : SETS * odd + SETS, :, :])

@@ -25,7 +25,7 @@ def tile_pairwiserelationmodule_pa_kernel(tc, objs, W1, b1, W2, b2, out_0, out_1
     nc = tc.nc
     with tc.tile_pool(name="sbuf", bufs=1) as sbuf, tc.psum_pool(name="work", bufs=WORK_BANKS) as work, tc.psum_pool(
         name="sums", bufs=1
-    ) as sums, tc.manual_schedule():
+    ) as sums:
 
         def bank():
             return work.tile([P, WIDTH], F32, tag="bank", name="bank")

@@ -18,6 +18,7 @@ TILES = 32
 GROUP = 4
 GROUPS = TILES // GROUP
 WORK_BANKS = 7
+VECTOR_GROUPS = 4
 FLOPS = 2 * SETS * OBJECTS * OBJECTS * (2 * WIDTH * WIDTH + WIDTH * WIDTH)
 
 
@@ -98,7 +99,8 @@ def tile_pairwiserelationmodule_pa_kernel(tc, objs, W1, b1, W2, b2, out_0, out_1
         quantise_half(w1_q[1], 1)
 
         a_sb = sbuf.tile([P, OBJECTS, SETS, PACK], F32)
-        b_sb = sbuf.tile([P, 4, SETS, 2, PACK], F32)
+        b_sb = sbuf.tile([P, 4, SETS, PACK], F32)
+        b_banks = {}
         b1_spread = b1_pt[:].rearrange("p u e -> p (u e)").unsqueeze(1).unsqueeze(1).to_broadcast([P, 2, SETS, PACK])
 
         def first_layer(half, kl):
@@ -115,15 +117,17 @@ def tile_pairwiserelationmodule_pa_kernel(tc, objs, W1, b1, W2, b2, out_0, out_1
                 )
             if half == 0:
                 nc.vector.tensor_tensor(
-                    out=a_sb[:, kl : OBJECTS : 4, :, :],
+                    out=a_sb[:, 2 * kl : 2 * kl + 2, :, :],
                     in0=acc[:].rearrange("p (t b h) -> p h b t", t=PACK, h=2),
                     in1=b1_spread,
                     op=ADD,
                 )
+            elif kl < 2:
+                b_banks[kl] = acc
             else:
                 nc.scalar.copy(
-                    out=b_sb[:, kl, :, :, :].rearrange("p b h t -> p (b h) t"),
-                    in_=acc[:].rearrange("p (t i) -> p i t", t=PACK),
+                    out=b_sb[:, 2 * (kl - 2) : 2 * (kl - 2) + 2, :, :],
+                    in_=acc[:].rearrange("p (t b h) -> p h b t", t=PACK, h=2),
                 )
 
         h_bf = [sbuf.tile([P, PACK * WIDTH], BF16, align_bytes=64, name="h_bf%d" % g) for g in range(GROUPS)]
@@ -132,19 +136,34 @@ def tile_pairwiserelationmodule_pa_kernel(tc, objs, W1, b1, W2, b2, out_0, out_1
         x_sb = [sbuf.tile([P, GROUP, WIDTH], F32, name="x_sb%d" % g) for g in range(GROUPS)]
         z_banks = {}
         sum_bank = sums.tile([P, WIDTH], F32)
-        out_rows = out_0.rearrange("b q n -> (b q) n").rearrange("(p t) n -> p t n", t=TILES)
+        out_rows = out_0.rearrange("b (k h j) n -> h b k j n", h=2, j=GROUP)
+        k_of_group = [4 * (g % 2) + g // 2 for g in range(GROUPS)]
 
         def exists(g):
             return 0 <= g < GROUPS
 
         def add_a_b(g):
-            if not exists(g):
+            if not 0 <= g < VECTOR_GROUPS:
                 return
+            nc.vector.tensor_tensor(
+                out=h_bf[g][:].rearrange("p (i b t) -> p i b t", i=OBJECTS, t=PACK),
+                in0=a_sb[:],
+                in1=b_banks[g // 2][:]
+                .rearrange("p (t b h) -> p h b t", t=PACK, h=2)[:, g % 2, :, :]
+                .unsqueeze(1)
+                .to_broadcast([P, OBJECTS, SETS, PACK]),
+                op=ADD,
+            )
+
+        def add_a_b_gpsimd(g):
             for j in range(GROUP):
-                nc.vector.tensor_tensor(
-                    out=h_bf[g][:, WIDTH * j : WIDTH * j + WIDTH].rearrange("p (b h t) -> p b h t", h=2, t=PACK),
-                    in0=a_sb[:, (GROUP * g + j) % OBJECTS, :, :].unsqueeze(2).to_broadcast([P, SETS, 2, PACK]),
-                    in1=b_sb[:, g // 2, :, :, :],
+                nc.gpsimd.tensor_tensor(
+                    out=h_bf[g][:, WIDTH * j : WIDTH * j + WIDTH].rearrange("p (i c) -> p i c", i=2),
+                    in0=a_sb[:, 2 * j : 2 * j + 2, :, :].rearrange("p i b t -> p i (b t)"),
+                    in1=b_sb[:, g - VECTOR_GROUPS, :, :]
+                    .rearrange("p b t -> p (b t)")
+                    .unsqueeze(1)
+                    .to_broadcast([P, 2, SETS * PACK]),
                     op=ADD,
                 )
 
@@ -178,7 +197,10 @@ def tile_pairwiserelationmodule_pa_kernel(tc, objs, W1, b1, W2, b2, out_0, out_1
             if not exists(g):
                 return
             nc.scalar.activation(out=x_sb[g][:, first:stop, :], in_=x_sb[g][:, first:stop, :], func=RELU)
-            nc.sync.dma_start(out=out_rows[:, GROUP * g + first : GROUP * g + stop, :], in_=x_sb[g][:, first:stop, :])
+            for h in range(2):
+                nc.sync.dma_start(
+                    out=out_rows[h][:, k_of_group[g], first:stop, :], in_=x_sb[g][SETS * h : SETS * h + SETS, first:stop, :]
+                )
             for j in range(first, stop):
                 for c in range(4):
                     nc.tensor.matmul(
@@ -202,6 +224,8 @@ def tile_pairwiserelationmodule_pa_kernel(tc, objs, W1, b1, W2, b2, out_0, out_1
         nc.scalar.copy(out=b2_spread[:], in_=b2_bank[:])
         for kl in range(1, 4):
             first_layer(1, kl)
+        for g in range(VECTOR_GROUPS, GROUPS):
+            add_a_b_gpsimd(g)
         relu_h(0)
         add_a_b(1)
         quantise_half(w2_q, 0)
@@ -224,8 +248,8 @@ def tile_pairwiserelationmodule_pa_kernel(tc, objs, W1, b1, W2, b2, out_0, out_1
 
         s_t = sbuf.tile([P, 4, SETS], F32)
         nc.vector.tensor_reduce(
-            out=s_t[:].rearrange("p c b -> p (c b)"),
-            in_=sum_bank[:].rearrange("p (i h) -> p i h", h=2),
+            out=s_t[:],
+            in_=sum_bank[:].rearrange("p (c h b) -> p c b h", c=4, h=2),
             axis=mybir.AxisListType.X,
             op=ADD,
         )

@@ -18,7 +18,11 @@ TILES = 32
 GROUP = 4
 GROUPS = TILES // GROUP
 WORK_BANKS = 7
-VECTOR_GROUPS = 4
+EARLY = 2
+GPSIMD_GROUPS = (4, 5, 6, 7)
+ORDER = (0, 4, 1, 5, 2, 6, 3, 7)
+VECTOR_RELU_GROUPS = (3, 7)
+ADD_AHEAD = 3
 FLOPS = 2 * SETS * OBJECTS * OBJECTS * (2 * WIDTH * WIDTH + WIDTH * WIDTH)
 
 
@@ -26,7 +30,7 @@ def tile_pairwiserelationmodule_pa_kernel(tc, objs, W1, b1, W2, b2, out_0, out_1
     nc = tc.nc
     with tc.tile_pool(name="sbuf", bufs=1) as sbuf, tc.psum_pool(name="work", bufs=WORK_BANKS) as work, tc.psum_pool(
         name="sums", bufs=1
-    ) as sums:
+    ) as sums, tc.manual_schedule():
 
         def bank():
             return work.tile([P, WIDTH], F32, tag="bank", name="bank")
@@ -59,7 +63,7 @@ def tile_pairwiserelationmodule_pa_kernel(tc, objs, W1, b1, W2, b2, out_0, out_1
                 sbuf.tile([P, WIDTH], U8, align_bytes=64, name=name + "_scales"),
             )
 
-        def transpose_half(rows_sb, first_word, side, dst, copy):
+        def transpose_half(rows_sb, first_word, side):
             planes = bank()
             for slot in range(2):
                 words = rows_sb[:, 2 * side + slot, :].bitcast(F32)
@@ -69,7 +73,10 @@ def tile_pairwiserelationmodule_pa_kernel(tc, objs, W1, b1, W2, b2, out_0, out_1
                         words[:, first_word + P * u : first_word + P * u + P],
                         identity[:],
                     )
-            copy(
+            return planes
+
+        def copy_half(planes, dst, side):
+            nc.scalar.copy(
                 out=dst[0][:, 1024 * side : 1024 * side + 1024].bitcast(F32).rearrange("p (s c u) -> p s c u", s=2, u=2),
                 in_=planes[:].rearrange("p (s u c) -> p s c u", s=2, u=2),
             )
@@ -85,23 +92,10 @@ def tile_pairwiserelationmodule_pa_kernel(tc, objs, W1, b1, W2, b2, out_0, out_1
         w1_q = [operand("w1a"), operand("w1b")]
         w2_q = operand("w2")
 
-        transpose_half(objs_sb, 0, 0, objs_q, nc.scalar.copy)
-        transpose_half(objs_sb, 0, 1, objs_q, nc.vector.tensor_copy)
-        transpose_half(w1_sb, 0, 0, w1_q[0], nc.scalar.copy)
-        quantise_half(objs_q, 0)
-        transpose_half(w1_sb, 0, 1, w1_q[0], nc.vector.tensor_copy)
-        quantise_half(objs_q, 1)
-        quantise_half(w1_q[0], 0)
-        quantise_half(w1_q[0], 1)
-        transpose_half(w1_sb, 256, 0, w1_q[1], nc.scalar.copy)
-        transpose_half(w1_sb, 256, 1, w1_q[1], nc.vector.tensor_copy)
-        quantise_half(w1_q[1], 0)
-        quantise_half(w1_q[1], 1)
-
         a_sb = sbuf.tile([P, OBJECTS, SETS, PACK], F32)
-        b_sb = sbuf.tile([P, 4, SETS, PACK], F32)
-        b_banks = {}
+        b_sb = sbuf.tile([P, 4, SETS, 2, PACK], F32)
         b1_spread = b1_pt[:].rearrange("p u e -> p (u e)").unsqueeze(1).unsqueeze(1).to_broadcast([P, 2, SETS, PACK])
+        l1_banks = {}
 
         def first_layer(half, kl):
             acc = bank()
@@ -115,20 +109,21 @@ def tile_pairwiserelationmodule_pa_kernel(tc, objs, W1, b1, W2, b2, out_0, out_1
                     start=True,
                     stop=True,
                 )
-            if half == 0:
-                nc.vector.tensor_tensor(
-                    out=a_sb[:, 2 * kl : 2 * kl + 2, :, :],
-                    in0=acc[:].rearrange("p (t b h) -> p h b t", t=PACK, h=2),
-                    in1=b1_spread,
-                    op=ADD,
-                )
-            elif kl < 2:
-                b_banks[kl] = acc
-            else:
-                nc.scalar.copy(
-                    out=b_sb[:, 2 * (kl - 2) : 2 * (kl - 2) + 2, :, :],
-                    in_=acc[:].rearrange("p (t b h) -> p h b t", t=PACK, h=2),
-                )
+            l1_banks[(half, kl)] = acc
+
+        def keep_a(kl):
+            nc.vector.tensor_tensor(
+                out=a_sb[:, kl : OBJECTS : 4, :, :],
+                in0=l1_banks[(0, kl)][:].rearrange("p (t b h) -> p h b t", t=PACK, h=2),
+                in1=b1_spread,
+                op=ADD,
+            )
+
+        def keep_b(kl):
+            nc.scalar.copy(
+                out=b_sb[:, kl, :, :, :].rearrange("p b h t -> p (b h) t"),
+                in_=l1_banks[(1, kl)][:].rearrange("p (t i) -> p i t", t=PACK),
+            )
 
         h_bf = [sbuf.tile([P, PACK * WIDTH], BF16, align_bytes=64, name="h_bf%d" % g) for g in range(GROUPS)]
         h_words = [sbuf.tile([P, WIDTH], U32, align_bytes=64, name="h_words%d" % g) for g in range(GROUPS)]
@@ -136,48 +131,32 @@ def tile_pairwiserelationmodule_pa_kernel(tc, objs, W1, b1, W2, b2, out_0, out_1
         x_sb = [sbuf.tile([P, GROUP, WIDTH], F32, name="x_sb%d" % g) for g in range(GROUPS)]
         z_banks = {}
         sum_bank = sums.tile([P, WIDTH], F32)
-        out_rows = out_0.rearrange("b (k h j) n -> h b k j n", h=2, j=GROUP)
-        k_of_group = [4 * (g % 2) + g // 2 for g in range(GROUPS)]
+        out_rows = out_0.rearrange("b q n -> (b q) n").rearrange("(p t) n -> p t n", t=TILES)
 
-        def exists(g):
-            return 0 <= g < GROUPS
-
-        def add_a_b(g):
-            if not 0 <= g < VECTOR_GROUPS:
-                return
-            nc.vector.tensor_tensor(
-                out=h_bf[g][:].rearrange("p (i b t) -> p i b t", i=OBJECTS, t=PACK),
-                in0=a_sb[:],
-                in1=b_banks[g // 2][:]
-                .rearrange("p (t b h) -> p h b t", t=PACK, h=2)[:, g % 2, :, :]
-                .unsqueeze(1)
-                .to_broadcast([P, OBJECTS, SETS, PACK]),
-                op=ADD,
-            )
-
-        def add_a_b_gpsimd(g):
-            for j in range(GROUP):
-                nc.gpsimd.tensor_tensor(
-                    out=h_bf[g][:, WIDTH * j : WIDTH * j + WIDTH].rearrange("p (i c) -> p i c", i=2),
-                    in0=a_sb[:, 2 * j : 2 * j + 2, :, :].rearrange("p i b t -> p i (b t)"),
-                    in1=b_sb[:, g - VECTOR_GROUPS, :, :]
-                    .rearrange("p b t -> p (b t)")
-                    .unsqueeze(1)
-                    .to_broadcast([P, 2, SETS * PACK]),
-                    op=ADD,
+        def add_a_b(g, j):
+            out = h_bf[g][:, WIDTH * j : WIDTH * j + WIDTH].rearrange("p (b h t) -> p b h t", h=2, t=PACK)
+            in0 = a_sb[:, (GROUP * g + j) % OBJECTS, :, :].unsqueeze(2).to_broadcast([P, SETS, 2, PACK])
+            if g in GPSIMD_GROUPS:
+                nc.gpsimd.tensor_tensor(out=out, in0=in0, in1=b_sb[:, g // 2, :, :, :], op=ADD)
+            else:
+                nc.vector.tensor_tensor(
+                    out=out, in0=in0, in1=l1_banks[(1, g // 2)][:].rearrange("p (t b h) -> p b h t", t=PACK, h=2), op=ADD
                 )
 
+        def relu_h_tile(g, j):
+            part = h_bf[g][:, WIDTH * j : WIDTH * j + WIDTH]
+            nc.scalar.activation(out=part, in_=part, func=RELU)
+
         def relu_h(g):
-            if exists(g):
+            if g in VECTOR_RELU_GROUPS:
+                nc.vector.tensor_scalar_max(out=h_bf[g][:], in0=h_bf[g][:], scalar1=0.0)
+            else:
                 nc.scalar.activation(out=h_bf[g][:], in_=h_bf[g][:], func=RELU)
 
         def quantise_h(g):
-            if exists(g):
-                nc.vector.quantize_mx(out=h_words[g][:].bitcast(FP8X4), scales=h_scales[g][:], in_=h_bf[g][:])
+            nc.vector.quantize_mx(out=h_words[g][:].bitcast(FP8X4), scales=h_scales[g][:], in_=h_bf[g][:])
 
         def second_layer(g, j):
-            if not exists(g):
-                return
             z_banks[(g, j)] = bank()
             nc.tensor.matmul_mx(
                 out=z_banks[(g, j)][:],
@@ -190,66 +169,92 @@ def tile_pairwiserelationmodule_pa_kernel(tc, objs, W1, b1, W2, b2, out_0, out_1
             )
 
         def add_b2(g, j):
-            if exists(g):
-                nc.vector.tensor_tensor(out=x_sb[g][:, j, :], in0=z_banks[(g, j)][:], in1=b2_spread[:], op=ADD)
+            nc.vector.tensor_tensor(out=x_sb[g][:, j, :], in0=z_banks[(g, j)][:], in1=b2_spread[:], op=ADD)
+
+        summed = []
 
         def relu_store_sum(g, first, stop):
-            if not exists(g):
-                return
             nc.scalar.activation(out=x_sb[g][:, first:stop, :], in_=x_sb[g][:, first:stop, :], func=RELU)
-            for h in range(2):
-                nc.sync.dma_start(
-                    out=out_rows[h][:, k_of_group[g], first:stop, :], in_=x_sb[g][SETS * h : SETS * h + SETS, first:stop, :]
-                )
+            nc.sync.dma_start(out=out_rows[:, GROUP * g + first : GROUP * g + stop, :], in_=x_sb[g][:, first:stop, :])
             for j in range(first, stop):
                 for c in range(4):
+                    summed.append((g, j, c))
                     nc.tensor.matmul(
                         out=sum_bank[:, P * c : P * c + P],
                         lhsT=x_sb[g][:, j, P * c : P * c + P],
                         rhs=identity[:],
                         is_transpose=True,
-                        start=(g == 0 and j == 0 and c == 0),
-                        stop=(g == GROUPS - 1 and j == GROUP - 1 and c == 3),
+                        start=(len(summed) == 1),
+                        stop=(len(summed) == 4 * TILES),
                     )
 
+        halves = [(objs_sb, 0, 0, objs_q), (objs_sb, 0, 1, objs_q), (w1_sb, 0, 0, w1_q[0]), (w1_sb, 0, 1, w1_q[0])]
+        halves += [(w1_sb, 256, 0, w1_q[1]), (w1_sb, 256, 1, w1_q[1])]
+        for n in range(len(halves)):
+            rows_sb, first_word, side, dst = halves[n]
+            copy_half(transpose_half(rows_sb, first_word, side), dst, side)
+            if n > 0:
+                quantise_half(halves[n - 1][3], halves[n - 1][2])
+        vector_groups = [g for g in ORDER if g not in GPSIMD_GROUPS]
+        gpsimd_groups = [g for g in ORDER if g in GPSIMD_GROUPS]
+        first = vector_groups[0]
         for kl in range(4):
             first_layer(0, kl)
-        first_layer(1, 0)
-        add_a_b(0)
-        transpose_half(w2_sb, 0, 0, w2_q, nc.scalar.copy)
-        transpose_half(w2_sb, 0, 1, w2_q, nc.scalar.copy)
+        keep_a(0)
+        quantise_half(w1_q[1], 1)
+        first_layer(1, first // 2)
+        first_layer(1, gpsimd_groups[0] // 2)
+        keep_b(gpsimd_groups[0] // 2)
+        add_a_b(first, 0)
+        relu_h_tile(first, 0)
+        w2_planes = [transpose_half(w2_sb, 0, 0), transpose_half(w2_sb, 0, 1)]
+        for j in range(1, GROUP):
+            keep_a(j)
+            add_a_b(first, j)
+            relu_h_tile(first, j)
+            if j <= 2:
+                copy_half(w2_planes[j - 1], w2_q, j - 1)
+        for kl in range(4):
+            if (1, kl) not in l1_banks:
+                first_layer(1, kl)
+                if 2 * kl in GPSIMD_GROUPS:
+                    keep_b(kl)
         b2_bank = bank()
         nc.tensor.matmul(out=b2_bank[:], lhsT=ones[:], rhs=b2_row[:], start=True, stop=True)
         b2_spread = sbuf.tile([P, WIDTH], F32)
         nc.scalar.copy(out=b2_spread[:], in_=b2_bank[:])
-        for kl in range(1, 4):
-            first_layer(1, kl)
-        for g in range(VECTOR_GROUPS, GROUPS):
-            add_a_b_gpsimd(g)
-        relu_h(0)
-        add_a_b(1)
+        for g in gpsimd_groups:
+            for j in range(GROUP):
+                add_a_b(g, j)
         quantise_half(w2_q, 0)
         quantise_half(w2_q, 1)
 
+        waiting = vector_groups[1:]
         for i in range(-1, GROUPS):
-            quantise_h(i + 1)
-            for j in range(WORK_BANKS - GROUP):
-                second_layer(i + 1, j)
-            relu_h(i + 2)
+            if i + 1 < GROUPS:
+                quantise_h(ORDER[i + 1])
+                for j in range(EARLY):
+                    second_layer(ORDER[i + 1], j)
+            while waiting and ORDER.index(waiting[0]) <= i + ADD_AHEAD:
+                for j in range(GROUP):
+                    add_a_b(waiting[0], j)
+                waiting = waiting[1:]
+            if i + 2 < GROUPS:
+                relu_h(ORDER[i + 2])
             for j in range(GROUP):
-                add_b2(i, j)
-                if j == 0:
-                    second_layer(i + 1, GROUP - 1)
+                if i >= 0:
+                    add_b2(ORDER[i], j)
+                if i + 1 < GROUPS and EARLY + j < GROUP:
+                    second_layer(ORDER[i + 1], EARLY + j)
                 if i == GROUPS - 1:
-                    relu_store_sum(i, j, j + 1)
-                elif j % 2 == 1:
-                    relu_store_sum(i, j - 1, j + 1)
-            add_a_b(i + 3)
+                    relu_store_sum(ORDER[i], j, j + 1)
+                elif i >= 0 and j % 2 == 1:
+                    relu_store_sum(ORDER[i], j - 1, j + 1)
 
         s_t = sbuf.tile([P, 4, SETS], F32)
         nc.vector.tensor_reduce(
-            out=s_t[:],
-            in_=sum_bank[:].rearrange("p (c h b) -> p c b h", c=4, h=2),
+            out=s_t[:].rearrange("p c b -> p (c b)"),
+            in_=sum_bank[:].rearrange("p (i h) -> p i h", h=2),
             axis=mybir.AxisListType.X,
             op=ADD,
         )

@@ -19,9 +19,9 @@ GROUP = 4
 GROUPS = TILES // GROUP
 WORK_BANKS = 7
 EARLY = 2
-GPSIMD_GROUPS = (4, 5, 6, 7)
-ORDER = (0, 4, 1, 5, 2, 6, 3, 7)
-VECTOR_RELU_GROUPS = (3, 7)
+GPSIMD_GROUPS = (2, 3, 5, 6, 7)
+ORDER = (0, 2, 1, 3, 4, 6, 5, 7)
+VECTOR_RELU_GROUPS = (6, 5, 7)
 ADD_AHEAD = 3
 FLOPS = 2 * SETS * OBJECTS * OBJECTS * (2 * WIDTH * WIDTH + WIDTH * WIDTH)
 
@@ -41,13 +41,15 @@ def tile_pairwiserelationmodule_pa_kernel(tc, objs, W1, b1, W2, b2, out_0, out_1
         nc.gpsimd.memset(b2_row[:], 0.0)
         nc.scalar.dma_start(out=b2_row[0:1, :], in_=b2.rearrange("(o n) -> o n", o=1))
         objs_sb = sbuf.tile([P, 4, WIDTH], BF16)
-        nc.sync.dma_start(out=objs_sb[:], in_=objs.rearrange("b o d -> (b o) d").rearrange("(p l) d -> p l d", l=4))
+        objs_rows = objs.rearrange("b o d -> (b o) d").rearrange("(p l) d -> p l d", l=4)
+        nc.sync.dma_start(out=objs_sb[:, 0:2, :], in_=objs_rows[:, 0:2, :])
         w1_sb = sbuf.tile([P, 4, 2 * WIDTH], BF16)
         w1_rows = W1.rearrange("(u p e) c -> u p e c", u=2, e=2)
         for half in range(2):
             cols = slice(WIDTH * half, WIDTH * half + WIDTH)
             for u in range(2):
                 nc.sync.dma_start(out=w1_sb[:, 2 * u : 2 * u + 2, cols], in_=w1_rows[u][:, :, cols])
+        nc.sync.dma_start(out=objs_sb[:, 2:4, :], in_=objs_rows[:, 2:4, :])
         w2_sb = sbuf.tile([P, 4, WIDTH], BF16)
         nc.sync.dma_start(out=w2_sb[:], in_=W2.rearrange("(j p) c -> p j c", p=P))
 
@@ -188,7 +190,7 @@ def tile_pairwiserelationmodule_pa_kernel(tc, objs, W1, b1, W2, b2, out_0, out_1
                         stop=(len(summed) == 4 * TILES),
                     )
 
-        halves = [(objs_sb, 0, 0, objs_q), (objs_sb, 0, 1, objs_q), (w1_sb, 0, 0, w1_q[0]), (w1_sb, 0, 1, w1_q[0])]
+        halves = [(objs_sb, 0, 0, objs_q), (w1_sb, 0, 0, w1_q[0]), (w1_sb, 0, 1, w1_q[0])]
         halves += [(w1_sb, 256, 0, w1_q[1]), (w1_sb, 256, 1, w1_q[1])]
         for n in range(len(halves)):
             rows_sb, first_word, side, dst = halves[n]
@@ -198,26 +200,34 @@ def tile_pairwiserelationmodule_pa_kernel(tc, objs, W1, b1, W2, b2, out_0, out_1
         vector_groups = [g for g in ORDER if g not in GPSIMD_GROUPS]
         gpsimd_groups = [g for g in ORDER if g in GPSIMD_GROUPS]
         first = vector_groups[0]
-        for kl in range(4):
-            first_layer(0, kl)
+        first_layer(0, 0)
+        first_layer(0, 1)
+        copy_half(transpose_half(objs_sb, 0, 1), objs_q, 1)
         keep_a(0)
         quantise_half(w1_q[1], 1)
         first_layer(1, first // 2)
         first_layer(1, gpsimd_groups[0] // 2)
         keep_b(gpsimd_groups[0] // 2)
+        copy_half(transpose_half(w2_sb, 0, 0), w2_q, 0)
+        keep_a(1)
         add_a_b(first, 0)
         relu_h_tile(first, 0)
-        w2_planes = [transpose_half(w2_sb, 0, 0), transpose_half(w2_sb, 0, 1)]
-        for j in range(1, GROUP):
-            keep_a(j)
-            add_a_b(first, j)
-            relu_h_tile(first, j)
-            if j <= 2:
-                copy_half(w2_planes[j - 1], w2_q, j - 1)
+        quantise_half(objs_q, 1)
+        add_a_b(first, 1)
+        relu_h_tile(first, 1)
+        first_layer(0, 2)
+        first_layer(0, 3)
+        copy_half(transpose_half(w2_sb, 0, 1), w2_q, 1)
+        keep_a(2)
+        keep_a(3)
+        add_a_b(first, 2)
+        relu_h_tile(first, 2)
+        add_a_b(first, 3)
+        relu_h_tile(first, 3)
         for kl in range(4):
             if (1, kl) not in l1_banks:
                 first_layer(1, kl)
-                if 2 * kl in GPSIMD_GROUPS:
+                if 2 * kl in GPSIMD_GROUPS or 2 * kl + 1 in GPSIMD_GROUPS:
                     keep_b(kl)
         b2_bank = bank()
         nc.tensor.matmul(out=b2_bank[:], lhsT=ones[:], rhs=b2_row[:], start=True, stop=True)

@@ -19,9 +19,9 @@ GROUP = 4
 GROUPS = TILES // GROUP
 WORK_BANKS = 7
 EARLY = 2
-GPSIMD_GROUPS = (2, 3, 5, 6, 7)
-ORDER = (0, 2, 1, 3, 4, 6, 5, 7)
-VECTOR_RELU_GROUPS = (6, 5, 7)
+GPSIMD_GROUPS = (2, 3, 6, 7)
+ORDER = (0, 1, 4, 2, 5, 3, 6, 7)
+VECTOR_RELU_GROUPS = (3, 6, 7)
 ADD_AHEAD = 3
 FLOPS = 2 * SETS * OBJECTS * OBJECTS * (2 * WIDTH * WIDTH + WIDTH * WIDTH)
 

@@ -23,6 +23,7 @@ GPSIMD_GROUPS = (2, 3, 6, 7)
 ORDER = (0, 1, 4, 2, 5, 3, 6, 7)
 VECTOR_RELU_GROUPS = (3, 6, 7)
 ADD_AHEAD = 3
+WARM_UP = 4
 FLOPS = 2 * SETS * OBJECTS * OBJECTS * (2 * WIDTH * WIDTH + WIDTH * WIDTH)
 
 
@@ -56,7 +57,12 @@ def tile_pairwiserelationmodule_pa_kernel(tc, objs, W1, b1, W2, b2, out_0, out_1
         identity = sbuf.tile([P, P], F32)
         make_identity(nc, identity[:])
         ones = sbuf.tile([P, P], BF16)
-        nc.gpsimd.memset(ones[:], 1.0)
+        nc.vector.memset(ones[:], 1.0)
+        warm_rhs = sbuf.tile([P, WIDTH], BF16)
+        nc.vector.memset(warm_rhs[:], 1.0)
+        warm_bank = bank()
+        for r in range(WARM_UP):
+            nc.tensor.matmul(out=warm_bank[:], lhsT=ones[:], rhs=warm_rhs[:], start=True, stop=True)
 
         def operand(name):
             return (

@@ -182,7 +182,10 @@ def tile_pairwiserelationmodule_pa_kernel(tc, objs, W1, b1, W2, b2, out_0, out_1
         summed = []
 
         def relu_store_sum(g, first, stop):
-            nc.scalar.activation(out=x_sb[g][:, first:stop, :], in_=x_sb[g][:, first:stop, :], func=RELU)
+            if g == ORDER[GROUPS - 1] and first == GROUP - 1:
+                nc.vector.tensor_scalar_max(out=x_sb[g][:, first:stop, :], in0=x_sb[g][:, first:stop, :], scalar1=0.0)
+            else:
+                nc.scalar.activation(out=x_sb[g][:, first:stop, :], in_=x_sb[g][:, first:stop, :], func=RELU)
             nc.sync.dma_start(out=out_rows[:, GROUP * g + first : GROUP * g + stop, :], in_=x_sb[g][:, first:stop, :])
             for j in range(first, stop):
                 for c in range(4):
@@ -262,7 +265,7 @@ def tile_pairwiserelationmodule_pa_kernel(tc, objs, W1, b1, W2, b2, out_0, out_1
                     add_b2(ORDER[i], j)
                 if i + 1 < GROUPS and EARLY + j < GROUP:
                     second_layer(ORDER[i + 1], EARLY + j)
-                if i == GROUPS - 1:
+                if i >= GROUPS - 2:
                     relu_store_sum(ORDER[i], j, j + 1)
                 elif i >= 0 and j % 2 == 1:
                     relu_store_sum(ORDER[i], j - 1, j + 1)

@@ -23,6 +23,23 @@ GPSIMD_GROUPS = (2, 3, 6, 7)
 ORDER = (0, 1, 4, 2, 5, 3, 6, 7)
 VECTOR_RELU_GROUPS = (3, 6, 7)
 ADD_AHEAD = 3
+V_KL = 0
+PE_KL = (2,)
+GP_KL = (1, 3)
+TILE = [
+    [(0, 0), (0, 1), (0, 4), (0, 5)],
+    [(0, 2), (0, 3), (0, 6), (0, 7)],
+    [(2, 0, 0), (2, 1, 0), (2, 0, 1), (2, 1, 1)],
+    [(1, 0), (1, 1), (1, 4), (1, 5)],
+    [(2, 2, 0), (2, 3, 0), (2, 2, 1), (2, 3, 1)],
+    [(1, 2), (1, 3), (1, 6), (1, 7)],
+    [(3, 0), (3, 1), (3, 4), (3, 5)],
+    [(3, 2), (3, 3), (3, 6), (3, 7)],
+]
+PE_RELU = "s"
+SUM_LAG = [4, 4, 4, 4, 4, 4, 2, 0]
+RELU_H = {3: "v", 5: "v", 6: "v", 7: "v"}
+RELU_X = ["ssss", "ssss", "ssss", "ssss", "ssss", "ssss", "ssss", "sssv"]
 WARM_UP = 4
 FLOPS = 2 * SETS * OBJECTS * OBJECTS * (2 * WIDTH * WIDTH + WIDTH * WIDTH)
 
@@ -41,6 +58,9 @@ def tile_pairwiserelationmodule_pa_kernel(tc, objs, W1, b1, W2, b2, out_0, out_1
         b2_row = sbuf.tile([P, WIDTH], BF16)
         nc.gpsimd.memset(b2_row[:], 0.0)
         nc.scalar.dma_start(out=b2_row[0:1, :], in_=b2.rearrange("(o n) -> o n", o=1))
+        b1_row = sbuf.tile([P, WIDTH], BF16)
+        nc.gpsimd.memset(b1_row[:], 0.0)
+        nc.scalar.dma_start(out=b1_row[0:1, :], in_=b1.rearrange("(o n) -> o n", o=1))
         objs_sb = sbuf.tile([P, 4, WIDTH], BF16)
         objs_rows = objs.rearrange("b o d -> (b o) d").rearrange("(p l) d -> p l d", l=4)
         nc.sync.dma_start(out=objs_sb[:, 0:2, :], in_=objs_rows[:, 0:2, :])
@@ -56,6 +76,12 @@ def tile_pairwiserelationmodule_pa_kernel(tc, objs, W1, b1, W2, b2, out_0, out_1
 
         identity = sbuf.tile([P, P], F32)
         make_identity(nc, identity[:])
+        swap = sbuf.tile([P, P], F32)
+        for d in range(2):
+            nc.gpsimd.tensor_copy(
+                out=swap[:].rearrange("p (b d) -> p b d", d=2)[:, :, d],
+                in_=identity[:].rearrange("p (b d) -> p b d", d=2)[:, :, 1 - d],
+            )
         ones = sbuf.tile([P, P], BF16)
         nc.vector.memset(ones[:], 1.0)
         warm_rhs = sbuf.tile([P, WIDTH], BF16)
@@ -101,11 +127,12 @@ def tile_pairwiserelationmodule_pa_kernel(tc, objs, W1, b1, W2, b2, out_0, out_1
         w2_q = operand("w2")
 
         a_sb = sbuf.tile([P, OBJECTS, SETS, PACK], F32)
-        b_sb = sbuf.tile([P, 4, SETS, 2, PACK], F32)
-        b1_spread = b1_pt[:].rearrange("p u e -> p (u e)").unsqueeze(1).unsqueeze(1).to_broadcast([P, 2, SETS, PACK])
-        l1_banks = {}
+        b_sb = {kl: sbuf.tile([P, SETS, 2, PACK], F32, name="b_sb%d" % kl) for kl in GP_KL}
+        a_rows = [sbuf.tile([P, WIDTH], F32, name="a_rows%d" % i) for i in range(4)]
+        b_rows = {kl: sbuf.tile([P, WIDTH], F32, name="b_rows%d" % kl) for kl in PE_KL}
+        b1_cols = b1_pt[:].rearrange("p u e -> p (u e)").unsqueeze(1).unsqueeze(1).to_broadcast([P, 2, SETS, PACK])
 
-        def first_layer(half, kl):
+        def columns(half, kl):
             acc = bank()
             for t in range(PACK):
                 nc.tensor.matmul_mx(
@@ -117,21 +144,43 @@ def tile_pairwiserelationmodule_pa_kernel(tc, objs, W1, b1, W2, b2, out_0, out_1
                     start=True,
                     stop=True,
                 )
-            l1_banks[(half, kl)] = acc
+            return acc
 
-        def keep_a(kl):
+        def rows(half, kl):
+            acc = bank()
+            nc.tensor.matmul_mx(
+                out=acc[:],
+                lhsT=objs_q[1][:, P * kl : P * kl + P].bitcast(FP8X4),
+                lhsT_scale=objs_q[2][:, P * kl : P * kl + P],
+                rhs=w1_q[half][1][:].bitcast(FP8X4),
+                rhs_scale=w1_q[half][2][:],
+                start=True,
+                stop=True,
+            )
+            return acc
+
+        def keep_a(kl, acc):
             nc.vector.tensor_tensor(
                 out=a_sb[:, kl : OBJECTS : 4, :, :],
-                in0=l1_banks[(0, kl)][:].rearrange("p (t b h) -> p h b t", t=PACK, h=2),
-                in1=b1_spread,
+                in0=acc[:].rearrange("p (t b h) -> p h b t", t=PACK, h=2),
+                in1=b1_cols,
                 op=ADD,
             )
 
-        def keep_b(kl):
+        def keep_b(kl, acc):
             nc.scalar.copy(
-                out=b_sb[:, kl, :, :, :].rearrange("p b h t -> p (b h) t"),
-                in_=l1_banks[(1, kl)][:].rearrange("p (t i) -> p i t", t=PACK),
+                out=b_sb[kl][:].rearrange("p b h t -> p (b h) t"),
+                in_=acc[:].rearrange("p (t i) -> p i t", t=PACK),
             )
+
+        def keep_a_rows(kl, acc, eng="s"):
+            if eng == "s":
+                nc.scalar.copy(out=a_rows[kl][:], in_=acc[:])
+            else:
+                nc.vector.tensor_copy(out=a_rows[kl][:], in_=acc[:])
+
+        def keep_b_rows(kl, acc):
+            nc.vector.tensor_tensor(out=b_rows[kl][:], in0=acc[:], in1=b1_rows[:], op=ADD)
 
         h_bf = [sbuf.tile([P, PACK * WIDTH], BF16, align_bytes=64, name="h_bf%d" % g) for g in range(GROUPS)]
         h_words = [sbuf.tile([P, WIDTH], U32, align_bytes=64, name="h_words%d" % g) for g in range(GROUPS)]
@@ -139,65 +188,113 @@ def tile_pairwiserelationmodule_pa_kernel(tc, objs, W1, b1, W2, b2, out_0, out_1
         x_sb = [sbuf.tile([P, GROUP, WIDTH], F32, name="x_sb%d" % g) for g in range(GROUPS)]
         z_banks = {}
         sum_bank = sums.tile([P, WIDTH], F32)
-        out_rows = out_0.rearrange("b q n -> (b q) n").rearrange("(p t) n -> p t n", t=TILES)
+        out_rows = out_0.rearrange("b (h t) n -> (b h) t n", t=TILES)
+        out_pairs = out_0.rearrange("b (q two) n -> b q two n", two=2)
 
-        def add_a_b(g, j):
-            out = h_bf[g][:, WIDTH * j : WIDTH * j + WIDTH].rearrange("p (b h t) -> p b h t", h=2, t=PACK)
-            in0 = a_sb[:, (GROUP * g + j) % OBJECTS, :, :].unsqueeze(2).to_broadcast([P, SETS, 2, PACK])
-            if g in GPSIMD_GROUPS:
-                nc.gpsimd.tensor_tensor(out=out, in0=in0, in1=b_sb[:, g // 2, :, :, :], op=ADD)
+        def h_part(p, j):
+            return h_bf[p][:, WIDTH * j : WIDTH * j + WIDTH]
+
+        def gp_add(p, j, eng="g"):
+            kl, m = TILE[p][j]
+            out = h_part(p, j).rearrange("p (b h t) -> p b h t", h=2, t=PACK)
+            in0 = a_sb[:, m, :, :].unsqueeze(2).to_broadcast([P, SETS, 2, PACK])
+            (nc.gpsimd if eng == "g" else nc.vector).tensor_tensor(out=out, in0=in0, in1=b_sb[kl][:], op=ADD)
+
+        t_banks = {}
+
+        def pe_add(p, j):
+            kl, ml, e = TILE[p][j]
+            acc = bank()
+            for t in range(PACK):
+                cols = slice(P * t, P * t + P)
+                nc.tensor.matmul(out=acc[:, cols], lhsT=a_rows[ml][:, cols], rhs=(swap if e else identity)[:], is_transpose=True, start=True, stop=False)
+                nc.tensor.matmul(out=acc[:, cols], lhsT=b_rows[kl][:, cols], rhs=identity[:], is_transpose=True, start=False, stop=True)
+            t_banks[(p, j)] = acc
+
+        def pe_relu(p, j, eng="s"):
+            out = h_part(p, j).rearrange("p (i t) -> p i t", t=PACK)
+            in_ = t_banks[(p, j)][:].rearrange("p (t i) -> p i t", t=PACK)
+            if eng == "s":
+                nc.scalar.activation(out=out, in_=in_, func=RELU)
             else:
-                nc.vector.tensor_tensor(
-                    out=out, in0=in0, in1=l1_banks[(1, g // 2)][:].rearrange("p (t b h) -> p b h t", t=PACK, h=2), op=ADD
-                )
+                nc.vector.tensor_scalar_max(out=out, in0=in_, scalar1=0.0)
 
-        def relu_h_tile(g, j):
-            part = h_bf[g][:, WIDTH * j : WIDTH * j + WIDTH]
-            nc.scalar.activation(out=part, in_=part, func=RELU)
-
-        def relu_h(g):
-            if g in VECTOR_RELU_GROUPS:
-                nc.vector.tensor_scalar_max(out=h_bf[g][:], in0=h_bf[g][:], scalar1=0.0)
+        def relu_h(p, eng="v"):
+            if eng == "v":
+                nc.vector.tensor_scalar_max(out=h_bf[p][:], in0=h_bf[p][:], scalar1=0.0)
             else:
-                nc.scalar.activation(out=h_bf[g][:], in_=h_bf[g][:], func=RELU)
+                nc.scalar.activation(out=h_bf[p][:], in_=h_bf[p][:], func=RELU)
 
-        def quantise_h(g):
-            nc.vector.quantize_mx(out=h_words[g][:].bitcast(FP8X4), scales=h_scales[g][:], in_=h_bf[g][:])
+        def quantise_h(p):
+            nc.vector.quantize_mx(out=h_words[p][:].bitcast(FP8X4), scales=h_scales[p][:], in_=h_bf[p][:])
 
-        def second_layer(g, j):
-            z_banks[(g, j)] = bank()
+        def second_layer(p, j):
+            z_banks[(p, j)] = bank()
             nc.tensor.matmul_mx(
-                out=z_banks[(g, j)][:],
-                lhsT=h_words[g][:, P * j : P * j + P].bitcast(FP8X4),
-                lhsT_scale=h_scales[g][:, P * j : P * j + P],
+                out=z_banks[(p, j)][:],
+                lhsT=h_words[p][:, P * j : P * j + P].bitcast(FP8X4),
+                lhsT_scale=h_scales[p][:, P * j : P * j + P],
                 rhs=w2_q[1][:].bitcast(FP8X4),
                 rhs_scale=w2_q[2][:],
                 start=True,
                 stop=True,
             )
 
-        def add_b2(g, j):
-            nc.vector.tensor_tensor(out=x_sb[g][:, j, :], in0=z_banks[(g, j)][:], in1=b2_spread[:], op=ADD)
+        def add_b2(p, j):
+            nc.vector.tensor_tensor(out=x_sb[p][:, j, :], in0=z_banks[(p, j)][:], in1=b2_rows[:], op=ADD)
 
         summed = []
 
-        def relu_store_sum(g, first, stop):
-            if g == ORDER[GROUPS - 1] and first == GROUP - 1:
-                nc.vector.tensor_scalar_max(out=x_sb[g][:, first:stop, :], in0=x_sb[g][:, first:stop, :], scalar1=0.0)
+        def relu_x(p, first, stop, eng):
+            part = x_sb[p][:, first:stop, :]
+            if eng == "s":
+                nc.scalar.activation(out=part, in_=part, func=RELU)
+            elif eng == "v":
+                nc.vector.tensor_scalar_max(out=part, in0=part, scalar1=0.0)
             else:
-                nc.scalar.activation(out=x_sb[g][:, first:stop, :], in_=x_sb[g][:, first:stop, :], func=RELU)
-            nc.sync.dma_start(out=out_rows[:, GROUP * g + first : GROUP * g + stop, :], in_=x_sb[g][:, first:stop, :])
-            for j in range(first, stop):
-                for c in range(4):
-                    summed.append((g, j, c))
-                    nc.tensor.matmul(
-                        out=sum_bank[:, P * c : P * c + P],
-                        lhsT=x_sb[g][:, j, P * c : P * c + P],
-                        rhs=identity[:],
-                        is_transpose=True,
-                        start=(len(summed) == 1),
-                        stop=(len(summed) == 4 * TILES),
-                    )
+                nc.gpsimd.tensor_scalar(out=part, in0=part, scalar1=3.0e38, scalar2=0.0, op0=mybir.AluOpType.min, op1=mybir.AluOpType.max)
+
+        def store(p, first, stop):
+            if len(TILE[p][0]) == 2:
+                kl, m = TILE[p][first]
+                nc.sync.dma_start(out=out_rows[:, OBJECTS * kl + m : OBJECTS * kl + m + stop - first, :], in_=x_sb[p][:, first:stop, :])
+            else:
+                kl, ml, e = TILE[p][first]
+                for d in range(2):
+                    q = 8 * (4 * d + kl) + 4 * (d if e == 0 else 1 - d) + ml
+                    nc.sync.dma_start(out=out_0[:, q : q + stop - first, :], in_=x_sb[p][d : P : 2, first:stop, :])
+
+        def sum_tile(p, j):
+            for c in range(4):
+                summed.append((p, j, c))
+                nc.tensor.matmul(
+                    out=sum_bank[:, P * c : P * c + P],
+                    lhsT=x_sb[p][:, j, P * c : P * c + P],
+                    rhs=identity[:],
+                    is_transpose=True,
+                    start=(len(summed) == 1),
+                    stop=(len(summed) == 4 * TILES),
+                )
+
+        def spread(row):
+            acc = bank()
+            nc.tensor.matmul(out=acc[:], lhsT=ones[:], rhs=row, start=True, stop=True)
+            return acc
+
+        def v_add(p, j, acc):
+            kl, m = TILE[p][j]
+            nc.vector.tensor_tensor(
+                out=h_part(p, j).rearrange("p (b h t) -> p b h t", h=2, t=PACK),
+                in0=a_sb[:, m, :, :].unsqueeze(2).to_broadcast([P, SETS, 2, PACK]),
+                in1=acc[:].rearrange("p (t b h) -> p b h t", t=PACK, h=2),
+                op=ADD,
+            )
+
+        def relu_tile(p, j):
+            nc.scalar.activation(out=h_part(p, j), in_=h_part(p, j), func=RELU)
+
+        b1_rows = sbuf.tile([P, WIDTH], F32)
+        b2_rows = sbuf.tile([P, WIDTH], F32)
 
         halves = [(objs_sb, 0, 0, objs_q), (w1_sb, 0, 0, w1_q[0]), (w1_sb, 0, 1, w1_q[0])]
         halves += [(w1_sb, 256, 0, w1_q[1]), (w1_sb, 256, 1, w1_q[1])]
@@ -206,69 +303,92 @@ def tile_pairwiserelationmodule_pa_kernel(tc, objs, W1, b1, W2, b2, out_0, out_1
             copy_half(transpose_half(rows_sb, first_word, side), dst, side)
             if n > 0:
                 quantise_half(halves[n - 1][3], halves[n - 1][2])
-        vector_groups = [g for g in ORDER if g not in GPSIMD_GROUPS]
-        gpsimd_groups = [g for g in ORDER if g in GPSIMD_GROUPS]
-        first = vector_groups[0]
-        first_layer(0, 0)
-        first_layer(0, 1)
+        ac0 = columns(0, 0)
+        ac1 = columns(0, 1)
         copy_half(transpose_half(objs_sb, 0, 1), objs_q, 1)
-        keep_a(0)
+        keep_a(0, ac0)
         quantise_half(w1_q[1], 1)
-        first_layer(1, first // 2)
-        first_layer(1, gpsimd_groups[0] // 2)
-        keep_b(gpsimd_groups[0] // 2)
+        keep_a(1, ac1)
+        bc0 = columns(1, 0)
+        bc1 = columns(1, 1)
+        keep_b(1, bc1)
+        v_add(0, 0, bc0)
+        relu_tile(0, 0)
+        v_add(0, 1, bc0)
         copy_half(transpose_half(w2_sb, 0, 0), w2_q, 0)
-        keep_a(1)
-        add_a_b(first, 0)
-        relu_h_tile(first, 0)
+        relu_tile(0, 1)
         quantise_half(objs_q, 1)
-        add_a_b(first, 1)
-        relu_h_tile(first, 1)
-        first_layer(0, 2)
-        first_layer(0, 3)
+        v_add(0, 2, bc0)
         copy_half(transpose_half(w2_sb, 0, 1), w2_q, 1)
-        keep_a(2)
-        keep_a(3)
-        add_a_b(first, 2)
-        relu_h_tile(first, 2)
-        add_a_b(first, 3)
-        relu_h_tile(first, 3)
-        for kl in range(4):
-            if (1, kl) not in l1_banks:
-                first_layer(1, kl)
-                if 2 * kl in GPSIMD_GROUPS or 2 * kl + 1 in GPSIMD_GROUPS:
-                    keep_b(kl)
-        b2_bank = bank()
-        nc.tensor.matmul(out=b2_bank[:], lhsT=ones[:], rhs=b2_row[:], start=True, stop=True)
-        b2_spread = sbuf.tile([P, WIDTH], F32)
-        nc.scalar.copy(out=b2_spread[:], in_=b2_bank[:])
-        for g in gpsimd_groups:
-            for j in range(GROUP):
-                add_a_b(g, j)
+        relu_tile(0, 2)
+        v_add(0, 3, bc0)
+        relu_tile(0, 3)
+        for j in range(GROUP):
+            gp_add(3, j)
+        ac2 = columns(0, 2)
+        ac3 = columns(0, 3)
+        b1_acc = spread(b1_row[:].rearrange("o (u p e) -> o u e p", u=2, e=2))
+        nc.scalar.copy(out=b1_rows[:], in_=b1_acc[:])
         quantise_half(w2_q, 0)
+        keep_a(2, ac2)
         quantise_half(w2_q, 1)
-
-        waiting = vector_groups[1:]
+        keep_a(3, ac3)
+        quantise_h(0)
+        b2r = rows(1, 2)
+        for i in range(2):
+            keep_a_rows(i, rows(0, i))
+        second_layer(0, 0)
+        keep_b_rows(2, b2r)
+        for i in range(2, 4):
+            keep_a_rows(i, rows(0, i))
+        for j in range(GROUP):
+            v_add(1, j, bc0)
+        b2_acc = spread(b2_row[:])
+        nc.scalar.copy(out=b2_rows[:], in_=b2_acc[:])
+        second_layer(0, 1)
+        for j in range(GROUP):
+            pe_add(2, j)
+            pe_relu(2, j)
+        bc3 = columns(1, 3)
+        keep_b(3, bc3)
+        for p in (5, 6, 7):
+            for j in range(GROUP):
+                gp_add(p, j)
+        relu_h(1, "v")
+        T_AT = {0: [(4, 0), (4, 1)], 1: [(4, 2), (4, 3)]}
+        LAG = 2 * GROUP
+        to_sum = []
         for i in range(-1, GROUPS):
-            if i + 1 < GROUPS:
-                quantise_h(ORDER[i + 1])
+            nxt = i + 1
+            if nxt > 0 and nxt < GROUPS:
+                quantise_h(nxt)
+            if nxt < GROUPS:
                 for j in range(EARLY):
-                    second_layer(ORDER[i + 1], j)
-            while waiting and ORDER.index(waiting[0]) <= i + ADD_AHEAD:
-                for j in range(GROUP):
-                    add_a_b(waiting[0], j)
-                waiting = waiting[1:]
-            if i + 2 < GROUPS:
-                relu_h(ORDER[i + 2])
+                    if nxt > 0:
+                        second_layer(nxt, j)
+            if i + 2 in RELU_H:
+                relu_h(i + 2, RELU_H[i + 2])
             for j in range(GROUP):
                 if i >= 0:
-                    add_b2(ORDER[i], j)
-                if i + 1 < GROUPS and EARLY + j < GROUP:
-                    second_layer(ORDER[i + 1], EARLY + j)
-                if i >= GROUPS - 2:
-                    relu_store_sum(ORDER[i], j, j + 1)
-                elif i >= 0 and j % 2 == 1:
-                    relu_store_sum(ORDER[i], j - 1, j + 1)
+                    add_b2(i, j)
+                if nxt < GROUPS and EARLY + j < GROUP:
+                    second_layer(nxt, EARLY + j)
+                if j % 2 == 1:
+                    for p, jj in T_AT.get(i, [])[j // 2 : j // 2 + 1]:
+                        pe_add(p, jj)
+                if i >= 0:
+                    fine = i >= GROUPS - 2
+                    if fine or j % 2 == 1:
+                        f = j if fine else j - 1
+                        eng = RELU_X[i][j]
+                        relu_x(i, f, j + 1, eng)
+                        store(i, f, j + 1)
+                        to_sum += [(i, k) for k in range(f, j + 1)]
+                        while len(to_sum) > SUM_LAG[i]:
+                            sum_tile(*to_sum.pop(0))
+                if j % 2 == 1:
+                    for p, jj in T_AT.get(i, [])[j // 2 : j // 2 + 1]:
+                        pe_relu(p, jj, PE_RELU)
 
         s_t = sbuf.tile([P, 4, SETS], F32)
         nc.vector.tensor_reduce(

@@ -37,6 +37,20 @@ TILE = [
     [(3, 2), (3, 3), (3, 6), (3, 7)],
 ]
 PE_RELU = "s"
+FINE = 24
+BURST = 2
+HEAD = 10
+QUANT_AHEAD = 4
+V_ADD_AHEAD = 10
+RELU_AHEAD = 10
+PE_AHEAD = 13
+PE_EXIT = 1
+Z_AHEAD = 3
+SUM_AFTER = 3
+B_ROWS_AHEAD = 20
+GP_REST = (5, 6, 7)
+GP_SPLIT = 1
+RH_AT = 1
 SUM_LAG = [4, 4, 4, 4, 4, 4, 2, 0]
 RELU_H = {3: "v", 5: "v", 6: "v", 7: "v"}
 RELU_X = ["ssss", "ssss", "ssss", "ssss", "ssss", "ssss", "ssss", "sssv"]
@@ -56,10 +70,10 @@ def tile_pairwiserelationmodule_pa_kernel(tc, objs, W1, b1, W2, b2, out_0, out_1
         b1_pt = sbuf.tile([P, 2, 2], BF16)
         nc.scalar.dma_start(out=b1_pt[:], in_=b1.rearrange("(u p e) -> p u e", u=2, e=2))
         b2_row = sbuf.tile([P, WIDTH], BF16)
-        nc.gpsimd.memset(b2_row[:], 0.0)
+        nc.vector.memset(b2_row[:], 0.0)
         nc.scalar.dma_start(out=b2_row[0:1, :], in_=b2.rearrange("(o n) -> o n", o=1))
         b1_row = sbuf.tile([P, WIDTH], BF16)
-        nc.gpsimd.memset(b1_row[:], 0.0)
+        nc.vector.memset(b1_row[:], 0.0)
         nc.scalar.dma_start(out=b1_row[0:1, :], in_=b1.rearrange("(o n) -> o n", o=1))
         objs_sb = sbuf.tile([P, 4, WIDTH], BF16)
         objs_rows = objs.rearrange("b o d -> (b o) d").rearrange("(p l) d -> p l d", l=4)
@@ -109,8 +123,8 @@ def tile_pairwiserelationmodule_pa_kernel(tc, objs, W1, b1, W2, b2, out_0, out_1
                     )
             return planes
 
-        def copy_half(planes, dst, side):
-            nc.scalar.copy(
+        def copy_half(planes, dst, side, on_vector=False):
+            (nc.vector.tensor_copy if on_vector else nc.scalar.copy)(
                 out=dst[0][:, 1024 * side : 1024 * side + 1024].bitcast(F32).rearrange("p (s c u) -> p s c u", s=2, u=2),
                 in_=planes[:].rearrange("p (s u c) -> p s c u", s=2, u=2),
             )
@@ -198,7 +212,11 @@ def tile_pairwiserelationmodule_pa_kernel(tc, objs, W1, b1, W2, b2, out_0, out_1
             kl, m = TILE[p][j]
             out = h_part(p, j).rearrange("p (b h t) -> p b h t", h=2, t=PACK)
             in0 = a_sb[:, m, :, :].unsqueeze(2).to_broadcast([P, SETS, 2, PACK])
-            (nc.gpsimd if eng == "g" else nc.vector).tensor_tensor(out=out, in0=in0, in1=b_sb[kl][:], op=ADD)
+            step = SETS // GP_SPLIT
+            for s in range(0, SETS, step):
+                nc.gpsimd.tensor_tensor(
+                    out=out[:, s : s + step], in0=in0[:, s : s + step], in1=b_sb[kl][:, s : s + step], op=ADD
+                )
 
         t_banks = {}
 
@@ -221,7 +239,8 @@ def tile_pairwiserelationmodule_pa_kernel(tc, objs, W1, b1, W2, b2, out_0, out_1
 
         def relu_h(p, eng="v"):
             if eng == "v":
-                nc.vector.tensor_scalar_max(out=h_bf[p][:], in0=h_bf[p][:], scalar1=0.0)
+                n = WIDTH * len([t for t in TILE[p] if len(t) == 2])
+                nc.vector.tensor_scalar_max(out=h_bf[p][:, 0:n], in0=h_bf[p][:, 0:n], scalar1=0.0)
             else:
                 nc.scalar.activation(out=h_bf[p][:], in_=h_bf[p][:], func=RELU)
 
@@ -255,7 +274,7 @@ def tile_pairwiserelationmodule_pa_kernel(tc, objs, W1, b1, W2, b2, out_0, out_1
                 nc.gpsimd.tensor_scalar(out=part, in0=part, scalar1=3.0e38, scalar2=0.0, op0=mybir.AluOpType.min, op1=mybir.AluOpType.max)
 
         def store(p, first, stop):
-            if len(TILE[p][0]) == 2:
+            if len(TILE[p][first]) == 2:
                 kl, m = TILE[p][first]
                 nc.sync.dma_start(out=out_rows[:, OBJECTS * kl + m : OBJECTS * kl + m + stop - first, :], in_=x_sb[p][:, first:stop, :])
             else:
@@ -334,61 +353,60 @@ def tile_pairwiserelationmodule_pa_kernel(tc, objs, W1, b1, W2, b2, out_0, out_1
         quantise_half(w2_q, 1)
         keep_a(3, ac3)
         quantise_h(0)
-        b2r = rows(1, 2)
-        for i in range(2):
-            keep_a_rows(i, rows(0, i))
-        second_layer(0, 0)
-        keep_b_rows(2, b2r)
-        for i in range(2, 4):
-            keep_a_rows(i, rows(0, i))
-        for j in range(GROUP):
-            v_add(1, j, bc0)
         b2_acc = spread(b2_row[:])
         nc.scalar.copy(out=b2_rows[:], in_=b2_acc[:])
-        second_layer(0, 1)
-        for j in range(GROUP):
-            pe_add(2, j)
-            pe_relu(2, j)
+        for i in range(4):
+            keep_a_rows(i, rows(0, i))
+        for kl in PE_KL[:1]:
+            keep_b_rows(kl, rows(1, kl))
         bc3 = columns(1, 3)
         keep_b(3, bc3)
-        for p in (5, 6, 7):
+        for p in GP_REST:
             for j in range(GROUP):
                 gp_add(p, j)
-        relu_h(1, "v")
-        T_AT = {0: [(4, 0), (4, 1)], 1: [(4, 2), (4, 3)]}
-        LAG = 2 * GROUP
-        to_sum = []
-        for i in range(-1, GROUPS):
-            nxt = i + 1
-            if nxt > 0 and nxt < GROUPS:
-                quantise_h(nxt)
-            if nxt < GROUPS:
-                for j in range(EARLY):
-                    if nxt > 0:
-                        second_layer(nxt, j)
-            if i + 2 in RELU_H:
-                relu_h(i + 2, RELU_H[i + 2])
-            for j in range(GROUP):
-                if i >= 0:
-                    add_b2(i, j)
-                if nxt < GROUPS and EARLY + j < GROUP:
-                    second_layer(nxt, EARLY + j)
-                if j % 2 == 1:
-                    for p, jj in T_AT.get(i, [])[j // 2 : j // 2 + 1]:
-                        pe_add(p, jj)
-                if i >= 0:
-                    fine = i >= GROUPS - 2
-                    if fine or j % 2 == 1:
-                        f = j if fine else j - 1
-                        eng = RELU_X[i][j]
-                        relu_x(i, f, j + 1, eng)
-                        store(i, f, j + 1)
-                        to_sum += [(i, k) for k in range(f, j + 1)]
-                        while len(to_sum) > SUM_LAG[i]:
-                            sum_tile(*to_sum.pop(0))
-                if j % 2 == 1:
-                    for p, jj in T_AT.get(i, [])[j // 2 : j // 2 + 1]:
-                        pe_relu(p, jj, PE_RELU)
+
+        def pe_tile(n):
+            return 0 <= n < TILES and len(TILE[n // GROUP][0]) == 3
+
+        for n in range(-HEAD, TILES + SUM_AFTER):
+            m = n + QUANT_AHEAD
+            if 0 < m < TILES and m % GROUP == 0:
+                quantise_h(m // GROUP)
+            m = n + B_ROWS_AHEAD
+            if m == GROUP * 6 and len(PE_KL) > 1:
+                keep_b_rows(PE_KL[1], rows(1, PE_KL[1]))
+            m = n + V_ADD_AHEAD
+            if GROUP <= m < 2 * GROUP:
+                v_add(1, m % GROUP, bc0)
+            if 0 <= n < TILES:
+                add_b2(n // GROUP, n % GROUP)
+            m = n + RELU_AHEAD
+            if GROUP <= m < TILES and m % GROUP == GROUP - 1 and not pe_tile(m):
+                relu_h(m // GROUP, "v")
+            m = n + PE_AHEAD
+            if pe_tile(m):
+                pe_add(m // GROUP, m % GROUP)
+            if (n + Z_AHEAD) % BURST == 0:
+                for m in range(n + Z_AHEAD, n + Z_AHEAD + BURST):
+                    if 0 <= m < TILES:
+                        second_layer(m // GROUP, m % GROUP)
+            if (n - SUM_AFTER) % BURST == BURST - 1:
+                for m in range(n - SUM_AFTER - BURST + 1, n - SUM_AFTER + 1):
+                    if 0 <= m < TILES:
+                        sum_tile(m // GROUP, m % GROUP)
+            m = n + PE_AHEAD - PE_EXIT
+            if pe_tile(m):
+                pe_relu(m // GROUP, m % GROUP, PE_RELU)
+            if 0 <= n < TILES and (n % 2 == 1 or n >= FINE):
+                f = n if n >= FINE else n - 1
+                p = n // GROUP
+                e = RELU_X[p]
+                if e[f % GROUP] == e[n % GROUP]:
+                    relu_x(p, f % GROUP, n % GROUP + 1, e[n % GROUP])
+                else:
+                    relu_x(p, f % GROUP, n % GROUP, e[f % GROUP])
+                    relu_x(p, n % GROUP, n % GROUP + 1, e[n % GROUP])
+                store(p, f % GROUP, n % GROUP + 1)
 
         s_t = sbuf.tile([P, 4, SETS], F32)
         nc.vector.tensor_reduce(

@@ -36,14 +36,17 @@ TILE = [
     [(3, 0), (3, 1), (3, 4), (3, 5)],
     [(3, 2), (3, 3), (3, 6), (3, 7)],
 ]
+TAIL = 1
+P1_S = 1
+IDLE = (0, 1, 1, 1, 1)
 PE_RELU = "s"
 FINE = 24
 BURST = 2
 HEAD = 10
 QUANT_AHEAD = 4
-V_ADD_AHEAD = 10
+V_ADD_AHEAD = 12
 RELU_AHEAD = 10
-PE_AHEAD = 13
+PE_AHEAD = 12
 PE_EXIT = 1
 Z_AHEAD = 3
 SUM_AFTER = 3
@@ -292,7 +295,7 @@ def tile_pairwiserelationmodule_pa_kernel(tc, objs, W1, b1, W2, b2, out_0, out_1
                     rhs=identity[:],
                     is_transpose=True,
                     start=(len(summed) == 1),
-                    stop=(len(summed) == 4 * TILES),
+                    stop=(len(summed) == 4 * TILES - 4),
                 )
 
         def spread(row):
@@ -312,6 +315,10 @@ def tile_pairwiserelationmodule_pa_kernel(tc, objs, W1, b1, W2, b2, out_0, out_1
         def relu_tile(p, j):
             nc.scalar.activation(out=h_part(p, j), in_=h_part(p, j), func=RELU)
 
+        def idle(k):
+            for r in range(k):
+                nc.tensor.matmul(out=sum_bank[:], lhsT=ones[:], rhs=warm_rhs[:], start=True, stop=True)
+
         b1_rows = sbuf.tile([P, WIDTH], F32)
         b2_rows = sbuf.tile([P, WIDTH], F32)
 
@@ -320,17 +327,20 @@ def tile_pairwiserelationmodule_pa_kernel(tc, objs, W1, b1, W2, b2, out_0, out_1
         for n in range(len(halves)):
             rows_sb, first_word, side, dst = halves[n]
             copy_half(transpose_half(rows_sb, first_word, side), dst, side)
+            idle(IDLE[n])
             if n > 0:
                 quantise_half(halves[n - 1][3], halves[n - 1][2])
         ac0 = columns(0, 0)
         ac1 = columns(0, 1)
-        copy_half(transpose_half(objs_sb, 0, 1), objs_q, 1)
-        keep_a(0, ac0)
         quantise_half(w1_q[1], 1)
-        keep_a(1, ac1)
-        bc0 = columns(1, 0)
+        keep_a(0, ac0)
         bc1 = columns(1, 1)
+        bc0 = columns(1, 0)
         keep_b(1, bc1)
+        keep_a(1, ac1)
+        for j in range(GROUP):
+            gp_add(3, j)
+        copy_half(transpose_half(objs_sb, 0, 1), objs_q, 1)
         v_add(0, 0, bc0)
         relu_tile(0, 0)
         v_add(0, 1, bc0)
@@ -342,8 +352,6 @@ def tile_pairwiserelationmodule_pa_kernel(tc, objs, W1, b1, W2, b2, out_0, out_1
         relu_tile(0, 2)
         v_add(0, 3, bc0)
         relu_tile(0, 3)
-        for j in range(GROUP):
-            gp_add(3, j)
         ac2 = columns(0, 2)
         ac3 = columns(0, 3)
         b1_acc = spread(b1_row[:].rearrange("o (u p e) -> o u e p", u=2, e=2))
@@ -368,6 +376,8 @@ def tile_pairwiserelationmodule_pa_kernel(tc, objs, W1, b1, W2, b2, out_0, out_1
         def pe_tile(n):
             return 0 <= n < TILES and len(TILE[n // GROUP][0]) == 3
 
+        kl, m = TILE[GROUPS - 1][GROUP - 1]
+        last_rows = out_rows[:, OBJECTS * kl + m, :]
         for n in range(-HEAD, TILES + SUM_AFTER):
             m = n + QUANT_AHEAD
             if 0 < m < TILES and m % GROUP == 0:
@@ -378,10 +388,12 @@ def tile_pairwiserelationmodule_pa_kernel(tc, objs, W1, b1, W2, b2, out_0, out_1
             m = n + V_ADD_AHEAD
             if GROUP <= m < 2 * GROUP:
                 v_add(1, m % GROUP, bc0)
-            if 0 <= n < TILES:
+                if P1_S:
+                    relu_tile(1, m % GROUP)
+            if 0 <= n < TILES - 1:
                 add_b2(n // GROUP, n % GROUP)
             m = n + RELU_AHEAD
-            if GROUP <= m < TILES and m % GROUP == GROUP - 1 and not pe_tile(m):
+            if GROUP * (2 if P1_S else 1) <= m < TILES and m % GROUP == GROUP - 1 and not pe_tile(m):
                 relu_h(m // GROUP, "v")
             m = n + PE_AHEAD
             if pe_tile(m):
@@ -392,12 +404,12 @@ def tile_pairwiserelationmodule_pa_kernel(tc, objs, W1, b1, W2, b2, out_0, out_1
                         second_layer(m // GROUP, m % GROUP)
             if (n - SUM_AFTER) % BURST == BURST - 1:
                 for m in range(n - SUM_AFTER - BURST + 1, n - SUM_AFTER + 1):
-                    if 0 <= m < TILES:
+                    if 0 <= m < TILES - 1:
                         sum_tile(m // GROUP, m % GROUP)
             m = n + PE_AHEAD - PE_EXIT
             if pe_tile(m):
                 pe_relu(m // GROUP, m % GROUP, PE_RELU)
-            if 0 <= n < TILES and (n % 2 == 1 or n >= FINE):
+            if 0 <= n < TILES - 1 and (n % 2 == 1 or n >= FINE):
                 f = n if n >= FINE else n - 1
                 p = n // GROUP
                 e = RELU_X[p]
@@ -408,22 +420,61 @@ def tile_pairwiserelationmodule_pa_kernel(tc, objs, W1, b1, W2, b2, out_0, out_1
                     relu_x(p, n % GROUP, n % GROUP + 1, e[n % GROUP])
                 store(p, f % GROUP, n % GROUP + 1)
 
+        p, j = GROUPS - 1, GROUP - 1
+        last = x_sb[p][:, j, :]
+        half = [slice(0, 256), slice(256, 512)]
         s_t = sbuf.tile([P, 4, SETS], F32)
+        last_t = sbuf.tile([P, 4, SETS], F32)
+        s_sb = sbuf.tile([P, 2, P], F32)
+        s_rows = out_1.rearrange("b (pair odd n) -> odd b pair n", pair=2, odd=2)
+        for s in half:
+            nc.vector.tensor_tensor(out=last[:, s], in0=z_banks[(p, j)][:, s], in1=b2_rows[:, s], op=ADD)
+        for s in half:
+            nc.vector.tensor_scalar_max(out=last[:, s], in0=last[:, s], scalar1=0.0)
+            nc.sync.dma_start(out=last_rows[:, s], in_=last[:, s])
         nc.vector.tensor_reduce(
             out=s_t[:].rearrange("p c b -> p (c b)"),
             in_=sum_bank[:].rearrange("p (i h) -> p i h", h=2),
             axis=mybir.AxisListType.X,
             op=ADD,
         )
-        s_bank = bank()
+        turned = []
         for pair in range(2):
-            nc.tensor.transpose(
-                s_bank[:, P * pair : P * pair + P],
-                s_t[:, 2 * pair : 2 * pair + 2, :].rearrange("p c b -> p (c b)"),
-                identity[:],
+            acc = bank()
+            for c in range(2):
+                nc.tensor.transpose(acc[:, P * c : P * c + P], last[:, 256 * pair + P * c : 256 * pair + P * c + P], identity[:])
+            turned.append(acc)
+        s_banks = []
+        for pair in range(2):
+            acc = bank()
+            nc.tensor.matmul(
+                out=acc[:, 0:P],
+                lhsT=s_t[:, 2 * pair : 2 * pair + 2, :].rearrange("p c b -> p (c b)"),
+                rhs=identity[:],
+                is_transpose=True,
+                start=True,
+                stop=False,
             )
-        s_sb = sbuf.tile([P, 2, P], F32)
-        nc.vector.tensor_copy(out=s_sb[:].rearrange("p a n -> p (a n)"), in_=s_bank[:, 0 : 2 * P])
-        s_rows = out_1.rearrange("b (pair odd n) -> odd b pair n", pair=2, odd=2)
-        for odd in range(2):
-            nc.sync.dma_start(out=s_rows[odd], in_=s_sb[SETS * odd : SETS * odd + SETS, :, :])
+            s_banks.append(acc)
+        for pair in range(2):
+            nc.vector.tensor_reduce(
+                out=last_t[:, 2 * pair : 2 * pair + 2, :].rearrange("p c b -> p (c b)"),
+                in_=turned[pair][:, 0:256].rearrange("p (i h) -> p i h", h=2),
+                axis=mybir.AxisListType.X,
+                op=ADD,
+            )
+        for pair in range(2):
+            nc.tensor.matmul(
+                out=s_banks[pair][:, 0:P],
+                lhsT=last_t[:, 2 * pair : 2 * pair + 2, :].rearrange("p c b -> p (c b)"),
+                rhs=identity[:],
+                is_transpose=True,
+                start=False,
+                stop=True,
+            )
+            if pair == 0:
+                nc.scalar.copy(out=s_sb[:, pair, :], in_=s_banks[pair][:, 0:P])
+            else:
+                nc.vector.tensor_copy(out=s_sb[:, pair, :], in_=s_banks[pair][:, 0:P])
+            for odd in range(2):
+                nc.sync.dma_start(out=s_rows[odd][:, pair, :], in_=s_sb[SETS * odd : SETS * odd + SETS, pair, :])

@@ -26,19 +26,24 @@ ADD_AHEAD = 3
 V_KL = 0
 PE_KL = (2,)
 GP_KL = (1, 3)
-TILE = [
-    [(0, 0), (0, 1), (0, 4), (0, 5)],
-    [(0, 2), (0, 3), (0, 6), (0, 7)],
-    [(2, 0, 0), (2, 1, 0), (2, 0, 1), (2, 1, 1)],
-    [(1, 0), (1, 1), (1, 4), (1, 5)],
-    [(2, 2, 0), (2, 3, 0), (2, 2, 1), (2, 3, 1)],
-    [(1, 2), (1, 3), (1, 6), (1, 7)],
-    [(3, 0), (3, 1), (3, 4), (3, 5)],
-    [(3, 2), (3, 3), (3, 6), (3, 7)],
-]
+GRP = dict(
+    V0=[(0, 0), (0, 1), (0, 4), (0, 5)],
+    V1=[(0, 2), (0, 3), (0, 6), (0, 7)],
+    T0=[(2, 0, 0), (2, 1, 0), (2, 0, 1), (2, 1, 1)],
+    T1=[(2, 2, 0), (2, 3, 0), (2, 2, 1), (2, 3, 1)],
+    G0=[(1, 0), (1, 1), (1, 4), (1, 5)],
+    G1=[(1, 2), (1, 3), (1, 6), (1, 7)],
+    G2=[(3, 0), (3, 1), (3, 4), (3, 5)],
+    G3=[(3, 2), (3, 3), (3, 6), (3, 7)],
+)
+PLACES = ("V0", "V1", "T0", "G0", "T1", "G1", "G2", "G3")
+TILE = [GRP[x] for x in PLACES]
+V1 = PLACES.index("V1")
 TAIL = 1
-P1_S = 1
-IDLE = (0, 1, 1, 1, 1)
+P1_S = 0
+S_RELU = ()
+S_AHEAD = 9
+IDLE = (1, 1, 1, 1, 0)
 PE_RELU = "s"
 FINE = 24
 BURST = 2
@@ -48,7 +53,7 @@ V_ADD_AHEAD = 12
 RELU_AHEAD = 10
 PE_AHEAD = 12
 PE_EXIT = 1
-Z_AHEAD = 3
+Z_AHEAD = 2
 SUM_AFTER = 3
 B_ROWS_AHEAD = 20
 GP_REST = (5, 6, 7)
@@ -339,7 +344,7 @@ def tile_pairwiserelationmodule_pa_kernel(tc, objs, W1, b1, W2, b2, out_0, out_1
         keep_b(1, bc1)
         keep_a(1, ac1)
         for j in range(GROUP):
-            gp_add(3, j)
+            gp_add(PLACES.index("G0"), j)
         copy_half(transpose_half(objs_sb, 0, 1), objs_q, 1)
         v_add(0, 0, bc0)
         relu_tile(0, 0)
@@ -369,7 +374,7 @@ def tile_pairwiserelationmodule_pa_kernel(tc, objs, W1, b1, W2, b2, out_0, out_1
             keep_b_rows(kl, rows(1, kl))
         bc3 = columns(1, 3)
         keep_b(3, bc3)
-        for p in GP_REST:
+        for p in [p for p in range(GROUPS) if PLACES[p] in ("G1", "G2", "G3")]:
             for j in range(GROUP):
                 gp_add(p, j)
 
@@ -386,15 +391,18 @@ def tile_pairwiserelationmodule_pa_kernel(tc, objs, W1, b1, W2, b2, out_0, out_1
             if m == GROUP * 6 and len(PE_KL) > 1:
                 keep_b_rows(PE_KL[1], rows(1, PE_KL[1]))
             m = n + V_ADD_AHEAD
-            if GROUP <= m < 2 * GROUP:
-                v_add(1, m % GROUP, bc0)
+            if m // GROUP == V1:
+                v_add(V1, m % GROUP, bc0)
                 if P1_S:
-                    relu_tile(1, m % GROUP)
+                    relu_tile(V1, m % GROUP)
             if 0 <= n < TILES - 1:
                 add_b2(n // GROUP, n % GROUP)
             m = n + RELU_AHEAD
-            if GROUP * (2 if P1_S else 1) <= m < TILES and m % GROUP == GROUP - 1 and not pe_tile(m):
+            if GROUP <= m < TILES and not (P1_S and m // GROUP == V1) and m % GROUP == GROUP - 1 and not pe_tile(m) and m // GROUP not in S_RELU:
                 relu_h(m // GROUP, "v")
+            m = n + S_AHEAD
+            if m // GROUP in S_RELU:
+                relu_tile(m // GROUP, m % GROUP)
             m = n + PE_AHEAD
             if pe_tile(m):
                 pe_add(m // GROUP, m % GROUP)

@@ -44,6 +44,7 @@ P1_S = 0
 S_RELU = ()
 S_AHEAD = 9
 IDLE = (1, 1, 1, 1, 0)
+W1U = 1
 PE_RELU = "s"
 FINE = 24
 BURST = 2
@@ -88,10 +89,8 @@ def tile_pairwiserelationmodule_pa_kernel(tc, objs, W1, b1, W2, b2, out_0, out_1
         nc.sync.dma_start(out=objs_sb[:, 0:2, :], in_=objs_rows[:, 0:2, :])
         w1_sb = sbuf.tile([P, 4, 2 * WIDTH], BF16)
         w1_rows = W1.rearrange("(u p e) c -> u p e c", u=2, e=2)
-        for half in range(2):
-            cols = slice(WIDTH * half, WIDTH * half + WIDTH)
-            for u in range(2):
-                nc.sync.dma_start(out=w1_sb[:, 2 * u : 2 * u + 2, cols], in_=w1_rows[u][:, :, cols])
+        for u in range(2):
+            nc.sync.dma_start(out=w1_sb[:, 2 * u : 2 * u + 2, :], in_=w1_rows[u])
         nc.sync.dma_start(out=objs_sb[:, 2:4, :], in_=objs_rows[:, 2:4, :])
         w2_sb = sbuf.tile([P, 4, WIDTH], BF16)
         nc.sync.dma_start(out=w2_sb[:], in_=W2.rearrange("(j p) c -> p j c", p=P))
@@ -327,8 +326,8 @@ def tile_pairwiserelationmodule_pa_kernel(tc, objs, W1, b1, W2, b2, out_0, out_1
         b1_rows = sbuf.tile([P, WIDTH], F32)
         b2_rows = sbuf.tile([P, WIDTH], F32)
 
-        halves = [(objs_sb, 0, 0, objs_q), (w1_sb, 0, 0, w1_q[0]), (w1_sb, 0, 1, w1_q[0])]
-        halves += [(w1_sb, 256, 0, w1_q[1]), (w1_sb, 256, 1, w1_q[1])]
+        halves = [(objs_sb, 0, 0, objs_q), (w1_sb, 0, 0, w1_q[0]), (w1_sb, 256, 0, w1_q[1])]
+        halves += [(w1_sb, 0, 1, w1_q[0]), (w1_sb, 256, 1, w1_q[1])]
         for n in range(len(halves)):
             rows_sb, first_word, side, dst = halves[n]
             copy_half(transpose_half(rows_sb, first_word, side), dst, side)

import concourse.mybir as mybir
from concourse.masks import make_identity

F32 = mybir.dt.float32
BF16 = mybir.dt.bfloat16
U32 = mybir.dt.uint32
U8 = mybir.dt.uint8
FP8X4 = mybir.dt.float8_e4m3fn_x4
ADD = mybir.AluOpType.add
RELU = mybir.ActivationFunctionType.Relu

P = 128
SETS = 64
OBJECTS = 8
WIDTH = 512
PACK = 4
TILES = 32
GROUP = 4
GROUPS = TILES // GROUP
WORK_BANKS = 7
EARLY = 2
GPSIMD_GROUPS = (2, 3, 6, 7)
ORDER = (0, 1, 4, 2, 5, 3, 6, 7)
VECTOR_RELU_GROUPS = (3, 6, 7)
ADD_AHEAD = 3
V_KL = 0
PE_KL = (2,)
GP_KL = (1, 3)
GRP = dict(
    V0=[(0, 0), (0, 1), (0, 4), (0, 5)],
    V1=[(0, 2), (0, 3), (0, 6), (0, 7)],
    T0=[(2, 0, 0), (2, 1, 0), (2, 0, 1), (2, 1, 1)],
    T1=[(2, 2, 0), (2, 3, 0), (2, 2, 1), (2, 3, 1)],
    G0=[(1, 0), (1, 1), (1, 4), (1, 5)],
    G1=[(1, 2), (1, 3), (1, 6), (1, 7)],
    G2=[(3, 0), (3, 1), (3, 4), (3, 5)],
    G3=[(3, 2), (3, 3), (3, 6), (3, 7)],
)
PLACES = ("V0", "V1", "T0", "G0", "T1", "G1", "G2", "G3")
TILE = [GRP[x] for x in PLACES]
V1 = PLACES.index("V1")
TAIL = 1
P1_S = 0
S_RELU = ()
S_AHEAD = 9
IDLE = (1, 1, 1, 1, 0)
W1U = 1
PE_RELU = "s"
FINE = 24
BURST = 2
HEAD = 10
QUANT_AHEAD = 4
V_ADD_AHEAD = 12
RELU_AHEAD = 10
PE_AHEAD = 12
PE_EXIT = 1
Z_AHEAD = 2
SUM_AFTER = 3
B_ROWS_AHEAD = 20
GP_REST = (5, 6, 7)
GP_SPLIT = 1
RH_AT = 1
SUM_LAG = [4, 4, 4, 4, 4, 4, 2, 0]
RELU_H = {3: "v", 5: "v", 6: "v", 7: "v"}
RELU_X = ["ssss", "ssss", "ssss", "ssss", "ssss", "ssss", "ssss", "sssv"]
WARM_UP = 4
FLOPS = 2 * SETS * OBJECTS * OBJECTS * (2 * WIDTH * WIDTH + WIDTH * WIDTH)


def tile_pairwiserelationmodule_pa_kernel(tc, objs, W1, b1, W2, b2, out_0, out_1):
    nc = tc.nc
    with tc.tile_pool(name="sbuf", bufs=1) as sbuf, tc.psum_pool(name="work", bufs=WORK_BANKS) as work, tc.psum_pool(
        name="sums", bufs=1
    ) as sums, tc.manual_schedule():

        def bank():
            return work.tile([P, WIDTH], F32, tag="bank", name="bank")

        b1_pt = sbuf.tile([P, 2, 2], BF16)
        nc.scalar.dma_start(out=b1_pt[:], in_=b1.rearrange("(u p e) -> p u e", u=2, e=2))
        b2_row = sbuf.tile([P, WIDTH], BF16)
        nc.vector.memset(b2_row[:], 0.0)
        nc.scalar.dma_start(out=b2_row[0:1, :], in_=b2.rearrange("(o n) -> o n", o=1))
        b1_row = sbuf.tile([P, WIDTH], BF16)
        nc.vector.memset(b1_row[:], 0.0)
        nc.scalar.dma_start(out=b1_row[0:1, :], in_=b1.rearrange("(o n) -> o n", o=1))
        objs_sb = sbuf.tile([P, 4, WIDTH], BF16)
        objs_rows = objs.rearrange("b o d -> (b o) d").rearrange("(p l) d -> p l d", l=4)
        nc.sync.dma_start(out=objs_sb[:, 0:2, :], in_=objs_rows[:, 0:2, :])
        w1_sb = sbuf.tile([P, 4, 2 * WIDTH], BF16)
        w1_rows = W1.rearrange("(u p e) c -> u p e c", u=2, e=2)
        for u in range(2):
            nc.sync.dma_start(out=w1_sb[:, 2 * u : 2 * u + 2, :], in_=w1_rows[u])
        nc.sync.dma_start(out=objs_sb[:, 2:4, :], in_=objs_rows[:, 2:4, :])
        w2_sb = sbuf.tile([P, 4, WIDTH], BF16)
        nc.sync.dma_start(out=w2_sb[:], in_=W2.rearrange("(j p) c -> p j c", p=P))

        identity = sbuf.tile([P, P], F32)
        make_identity(nc, identity[:])
        swap = sbuf.tile([P, P], F32)
        for d in range(2):
            nc.gpsimd.tensor_copy(
                out=swap[:].rearrange("p (b d) -> p b d", d=2)[:, :, d],
                in_=identity[:].rearrange("p (b d) -> p b d", d=2)[:, :, 1 - d],
            )
        ones = sbuf.tile([P, P], BF16)
        nc.vector.memset(ones[:], 1.0)
        warm_rhs = sbuf.tile([P, WIDTH], BF16)
        nc.vector.memset(warm_rhs[:], 1.0)
        warm_bank = bank()
        for r in range(WARM_UP):
            nc.tensor.matmul(out=warm_bank[:], lhsT=ones[:], rhs=warm_rhs[:], start=True, stop=True)

        def operand(name):
            return (
                sbuf.tile([P, PACK * WIDTH], BF16, align_bytes=64, name=name + "_bf"),
                sbuf.tile([P, WIDTH], U32, align_bytes=64, name=name + "_words"),
                sbuf.tile([P, WIDTH], U8, align_bytes=64, name=name + "_scales"),
            )

        def transpose_half(rows_sb, first_word, side):
            planes = bank()
            for slot in range(2):
                words = rows_sb[:, 2 * side + slot, :].bitcast(F32)
                for u in range(2):
                    nc.tensor.transpose(
                        planes[:, (2 * slot + u) * P : (2 * slot + u + 1) * P],
                        words[:, first_word + P * u : first_word + P * u + P],
                        identity[:],
                    )
            return planes

        def copy_half(planes, dst, side, on_vector=False):
            (nc.vector.tensor_copy if on_vector else nc.scalar.copy)(
                out=dst[0][:, 1024 * side : 1024 * side + 1024].bitcast(F32).rearrange("p (s c u) -> p s c u", s=2, u=2),
                in_=planes[:].rearrange("p (s u c) -> p s c u", s=2, u=2),
            )

        def quantise_half(dst, side):
            nc.vector.quantize_mx(
                out=dst[1][:, 256 * side : 256 * side + 256].bitcast(FP8X4),
                scales=dst[2][:, 256 * side : 256 * side + 256],
                in_=dst[0][:, 1024 * side : 1024 * side + 1024],
            )

        objs_q = operand("objs")
        w1_q = [operand("w1a"), operand("w1b")]
        w2_q = operand("w2")

        a_sb = sbuf.tile([P, OBJECTS, SETS, PACK], F32)
        b_sb = {kl: sbuf.tile([P, SETS, 2, PACK], F32, name="b_sb%d" % kl) for kl in GP_KL}
        a_rows = [sbuf.tile([P, WIDTH], F32, name="a_rows%d" % i) for i in range(4)]
        b_rows = {kl: sbuf.tile([P, WIDTH], F32, name="b_rows%d" % kl) for kl in PE_KL}
        b1_cols = b1_pt[:].rearrange("p u e -> p (u e)").unsqueeze(1).unsqueeze(1).to_broadcast([P, 2, SETS, PACK])

        def columns(half, kl):
            acc = bank()
            for t in range(PACK):
                nc.tensor.matmul_mx(
                    out=acc[:, P * t : P * t + P],
                    lhsT=w1_q[half][1][:, P * t : P * t + P].bitcast(FP8X4),
                    lhsT_scale=w1_q[half][2][:, P * t : P * t + P],
                    rhs=objs_q[1][:, P * kl : P * kl + P].bitcast(FP8X4),
                    rhs_scale=objs_q[2][:, P * kl : P * kl + P],
                    start=True,
                    stop=True,
                )
            return acc

        def rows(half, kl):
            acc = bank()
            nc.tensor.matmul_mx(
                out=acc[:],
                lhsT=objs_q[1][:, P * kl : P * kl + P].bitcast(FP8X4),
                lhsT_scale=objs_q[2][:, P * kl : P * kl + P],
                rhs=w1_q[half][1][:].bitcast(FP8X4),
                rhs_scale=w1_q[half][2][:],
                start=True,
                stop=True,
            )
            return acc

        def keep_a(kl, acc):
            nc.vector.tensor_tensor(
                out=a_sb[:, kl : OBJECTS : 4, :, :],
                in0=acc[:].rearrange("p (t b h) -> p h b t", t=PACK, h=2),
                in1=b1_cols,
                op=ADD,
            )

        def keep_b(kl, acc):
            nc.scalar.copy(
                out=b_sb[kl][:].rearrange("p b h t -> p (b h) t"),
                in_=acc[:].rearrange("p (t i) -> p i t", t=PACK),
            )

        def keep_a_rows(kl, acc, eng="s"):
            if eng == "s":
                nc.scalar.copy(out=a_rows[kl][:], in_=acc[:])
            else:
                nc.vector.tensor_copy(out=a_rows[kl][:], in_=acc[:])

        def keep_b_rows(kl, acc):
            nc.vector.tensor_tensor(out=b_rows[kl][:], in0=acc[:], in1=b1_rows[:], op=ADD)

        h_bf = [sbuf.tile([P, PACK * WIDTH], BF16, align_bytes=64, name="h_bf%d" % g) for g in range(GROUPS)]
        h_words = [sbuf.tile([P, WIDTH], U32, align_bytes=64, name="h_words%d" % g) for g in range(GROUPS)]
        h_scales = [sbuf.tile([P, WIDTH], U8, align_bytes=64, name="h_scales%d" % g) for g in range(GROUPS)]
        x_sb = [sbuf.tile([P, GROUP, WIDTH], F32, name="x_sb%d" % g) for g in range(GROUPS)]
        z_banks = {}
        sum_bank = sums.tile([P, WIDTH], F32)
        out_rows = out_0.rearrange("b (h t) n -> (b h) t n", t=TILES)
        out_pairs = out_0.rearrange("b (q two) n -> b q two n", two=2)

        def h_part(p, j):
            return h_bf[p][:, WIDTH * j : WIDTH * j + WIDTH]

        def gp_add(p, j, eng="g"):
            kl, m = TILE[p][j]
            out = h_part(p, j).rearrange("p (b h t) -> p b h t", h=2, t=PACK)
            in0 = a_sb[:, m, :, :].unsqueeze(2).to_broadcast([P, SETS, 2, PACK])
            step = SETS // GP_SPLIT
            for s in range(0, SETS, step):
                nc.gpsimd.tensor_tensor(
                    out=out[:, s : s + step], in0=in0[:, s : s + step], in1=b_sb[kl][:, s : s + step], op=ADD
                )

        t_banks = {}

        def pe_add(p, j):
            kl, ml, e = TILE[p][j]
            acc = bank()
            for t in range(PACK):
                cols = slice(P * t, P * t + P)
                nc.tensor.matmul(out=acc[:, cols], lhsT=a_rows[ml][:, cols], rhs=(swap if e else identity)[:], is_transpose=True, start=True, stop=False)
                nc.tensor.matmul(out=acc[:, cols], lhsT=b_rows[kl][:, cols], rhs=identity[:], is_transpose=True, start=False, stop=True)
            t_banks[(p, j)] = acc

        def pe_relu(p, j, eng="s"):
            out = h_part(p, j).rearrange("p (i t) -> p i t", t=PACK)
            in_ = t_banks[(p, j)][:].rearrange("p (t i) -> p i t", t=PACK)
            if eng == "s":
                nc.scalar.activation(out=out, in_=in_, func=RELU)
            else:
                nc.vector.tensor_scalar_max(out=out, in0=in_, scalar1=0.0)

        def relu_h(p, eng="v"):
            if eng == "v":
                n = WIDTH * len([t for t in TILE[p] if len(t) == 2])
                nc.vector.tensor_scalar_max(out=h_bf[p][:, 0:n], in0=h_bf[p][:, 0:n], scalar1=0.0)
            else:
                nc.scalar.activation(out=h_bf[p][:], in_=h_bf[p][:], func=RELU)

        def quantise_h(p):
            nc.vector.quantize_mx(out=h_words[p][:].bitcast(FP8X4), scales=h_scales[p][:], in_=h_bf[p][:])

        def second_layer(p, j):
            z_banks[(p, j)] = bank()
            nc.tensor.matmul_mx(
                out=z_banks[(p, j)][:],
                lhsT=h_words[p][:, P * j : P * j + P].bitcast(FP8X4),
                lhsT_scale=h_scales[p][:, P * j : P * j + P],
                rhs=w2_q[1][:].bitcast(FP8X4),
                rhs_scale=w2_q[2][:],
                start=True,
                stop=True,
            )

        def add_b2(p, j):
            nc.vector.tensor_tensor(out=x_sb[p][:, j, :], in0=z_banks[(p, j)][:], in1=b2_rows[:], op=ADD)

        summed = []

        def relu_x(p, first, stop, eng):
            part = x_sb[p][:, first:stop, :]
            if eng == "s":
                nc.scalar.activation(out=part, in_=part, func=RELU)
            elif eng == "v":
                nc.vector.tensor_scalar_max(out=part, in0=part, scalar1=0.0)
            else:
                nc.gpsimd.tensor_scalar(out=part, in0=part, scalar1=3.0e38, scalar2=0.0, op0=mybir.AluOpType.min, op1=mybir.AluOpType.max)

        def store(p, first, stop):
            if len(TILE[p][first]) == 2:
                kl, m = TILE[p][first]
                nc.sync.dma_start(out=out_rows[:, OBJECTS * kl + m : OBJECTS * kl + m + stop - first, :], in_=x_sb[p][:, first:stop, :])
            else:
                kl, ml, e = TILE[p][first]
                for d in range(2):
                    q = 8 * (4 * d + kl) + 4 * (d if e == 0 else 1 - d) + ml
                    nc.sync.dma_start(out=out_0[:, q : q + stop - first, :], in_=x_sb[p][d : P : 2, first:stop, :])

        def sum_tile(p, j):
            for c in range(4):
                summed.append((p, j, c))
                nc.tensor.matmul(
                    out=sum_bank[:, P * c : P * c + P],
                    lhsT=x_sb[p][:, j, P * c : P * c + P],
                    rhs=identity[:],
                    is_transpose=True,
                    start=(len(summed) == 1),
                    stop=(len(summed) == 4 * TILES - 4),
                )

        def spread(row):
            acc = bank()
            nc.tensor.matmul(out=acc[:], lhsT=ones[:], rhs=row, start=True, stop=True)
            return acc

        def v_add(p, j, acc):
            kl, m = TILE[p][j]
            nc.vector.tensor_tensor(
                out=h_part(p, j).rearrange("p (b h t) -> p b h t", h=2, t=PACK),
                in0=a_sb[:, m, :, :].unsqueeze(2).to_broadcast([P, SETS, 2, PACK]),
                in1=acc[:].rearrange("p (t b h) -> p b h t", t=PACK, h=2),
                op=ADD,
            )

        def relu_tile(p, j):
            nc.scalar.activation(out=h_part(p, j), in_=h_part(p, j), func=RELU)

        def idle(k):
            for r in range(k):
                nc.tensor.matmul(out=sum_bank[:], lhsT=ones[:], rhs=warm_rhs[:], start=True, stop=True)

        b1_rows = sbuf.tile([P, WIDTH], F32)
        b2_rows = sbuf.tile([P, WIDTH], F32)

        halves = [(objs_sb, 0, 0, objs_q), (w1_sb, 0, 0, w1_q[0]), (w1_sb, 256, 0, w1_q[1])]
        halves += [(w1_sb, 0, 1, w1_q[0]), (w1_sb, 256, 1, w1_q[1])]
        for n in range(len(halves)):
            rows_sb, first_word, side, dst = halves[n]
            copy_half(transpose_half(rows_sb, first_word, side), dst, side)
            idle(IDLE[n])
            if n > 0:
                quantise_half(halves[n - 1][3], halves[n - 1][2])
        ac0 = columns(0, 0)
        ac1 = columns(0, 1)
        quantise_half(w1_q[1], 1)
        keep_a(0, ac0)
        bc1 = columns(1, 1)
        bc0 = columns(1, 0)
        keep_b(1, bc1)
        keep_a(1, ac1)
        for j in range(GROUP):
            gp_add(PLACES.index("G0"), j)
        copy_half(transpose_half(objs_sb, 0, 1), objs_q, 1)
        v_add(0, 0, bc0)
        relu_tile(0, 0)
        v_add(0, 1, bc0)
        copy_half(transpose_half(w2_sb, 0, 0), w2_q, 0)
        relu_tile(0, 1)
        quantise_half(objs_q, 1)
        v_add(0, 2, bc0)
        copy_half(transpose_half(w2_sb, 0, 1), w2_q, 1)
        relu_tile(0, 2)
        v_add(0, 3, bc0)
        relu_tile(0, 3)
        ac2 = columns(0, 2)
        ac3 = columns(0, 3)
        b1_acc = spread(b1_row[:].rearrange("o (u p e) -> o u e p", u=2, e=2))
        nc.scalar.copy(out=b1_rows[:], in_=b1_acc[:])
        quantise_half(w2_q, 0)
        keep_a(2, ac2)
        quantise_half(w2_q, 1)
        keep_a(3, ac3)
        quantise_h(0)
        b2_acc = spread(b2_row[:])
        nc.scalar.copy(out=b2_rows[:], in_=b2_acc[:])
        for i in range(4):
            keep_a_rows(i, rows(0, i))
        for kl in PE_KL[:1]:
            keep_b_rows(kl, rows(1, kl))
        bc3 = columns(1, 3)
        keep_b(3, bc3)
        for p in [p for p in range(GROUPS) if PLACES[p] in ("G1", "G2", "G3")]:
            for j in range(GROUP):
                gp_add(p, j)

        def pe_tile(n):
            return 0 <= n < TILES and len(TILE[n // GROUP][0]) == 3

        kl, m = TILE[GROUPS - 1][GROUP - 1]
        last_rows = out_rows[:, OBJECTS * kl + m, :]
        for n in range(-HEAD, TILES + SUM_AFTER):
            m = n + QUANT_AHEAD
            if 0 < m < TILES and m % GROUP == 0:
                quantise_h(m // GROUP)
            m = n + B_ROWS_AHEAD
            if m == GROUP * 6 and len(PE_KL) > 1:
                keep_b_rows(PE_KL[1], rows(1, PE_KL[1]))
            m = n + V_ADD_AHEAD
            if m // GROUP == V1:
                v_add(V1, m % GROUP, bc0)
                if P1_S:
                    relu_tile(V1, m % GROUP)
            if 0 <= n < TILES - 1:
                add_b2(n // GROUP, n % GROUP)
            m = n + RELU_AHEAD
            if GROUP <= m < TILES and not (P1_S and m // GROUP == V1) and m % GROUP == GROUP - 1 and not pe_tile(m) and m // GROUP not in S_RELU:
                relu_h(m // GROUP, "v")
            m = n + S_AHEAD
            if m // GROUP in S_RELU:
                relu_tile(m // GROUP, m % GROUP)
            m = n + PE_AHEAD
            if pe_tile(m):
                pe_add(m // GROUP, m % GROUP)
            if (n + Z_AHEAD) % BURST == 0:
                for m in range(n + Z_AHEAD, n + Z_AHEAD + BURST):
                    if 0 <= m < TILES:
                        second_layer(m // GROUP, m % GROUP)
            if (n - SUM_AFTER) % BURST == BURST - 1:
                for m in range(n - SUM_AFTER - BURST + 1, n - SUM_AFTER + 1):
                    if 0 <= m < TILES - 1:
                        sum_tile(m // GROUP, m % GROUP)
            m = n + PE_AHEAD - PE_EXIT
            if pe_tile(m):
                pe_relu(m // GROUP, m % GROUP, PE_RELU)
            if 0 <= n < TILES - 1 and (n % 2 == 1 or n >= FINE):
                f = n if n >= FINE else n - 1
                p = n // GROUP
                e = RELU_X[p]
                if e[f % GROUP] == e[n % GROUP]:
                    relu_x(p, f % GROUP, n % GROUP + 1, e[n % GROUP])
                else:
                    relu_x(p, f % GROUP, n % GROUP, e[f % GROUP])
                    relu_x(p, n % GROUP, n % GROUP + 1, e[n % GROUP])
                store(p, f % GROUP, n % GROUP + 1)

        p, j = GROUPS - 1, GROUP - 1
        last = x_sb[p][:, j, :]
        half = [slice(0, 256), slice(256, 512)]
        s_t = sbuf.tile([P, 4, SETS], F32)
        last_t = sbuf.tile([P, 4, SETS], F32)
        s_sb = sbuf.tile([P, 2, P], F32)
        s_rows = out_1.rearrange("b (pair odd n) -> odd b pair n", pair=2, odd=2)
        for s in half:
            nc.vector.tensor_tensor(out=last[:, s], in0=z_banks[(p, j)][:, s], in1=b2_rows[:, s], op=ADD)
        for s in half:
            nc.vector.tensor_scalar_max(out=last[:, s], in0=last[:, s], scalar1=0.0)
            nc.sync.dma_start(out=last_rows[:, s], in_=last[:, s])
        nc.vector.tensor_reduce(
            out=s_t[:].rearrange("p c b -> p (c b)"),
            in_=sum_bank[:].rearrange("p (i h) -> p i h", h=2),
            axis=mybir.AxisListType.X,
            op=ADD,
        )
        turned = []
        for pair in range(2):
            acc = bank()
            for c in range(2):
                nc.tensor.transpose(acc[:, P * c : P * c + P], last[:, 256 * pair + P * c : 256 * pair + P * c + P], identity[:])
            turned.append(acc)
        s_banks = []
        for pair in range(2):
            acc = bank()
            nc.tensor.matmul(
                out=acc[:, 0:P],
                lhsT=s_t[:, 2 * pair : 2 * pair + 2, :].rearrange("p c b -> p (c b)"),
                rhs=identity[:],
                is_transpose=True,
                start=True,
                stop=False,
            )
            s_banks.append(acc)
        for pair in range(2):
            nc.vector.tensor_reduce(
                out=last_t[:, 2 * pair : 2 * pair + 2, :].rearrange("p c b -> p (c b)"),
                in_=turned[pair][:, 0:256].rearrange("p (i h) -> p i h", h=2),
                axis=mybir.AxisListType.X,
                op=ADD,
            )
        for pair in range(2):
            nc.tensor.matmul(
                out=s_banks[pair][:, 0:P],
                lhsT=last_t[:, 2 * pair : 2 * pair + 2, :].rearrange("p c b -> p (c b)"),
                rhs=identity[:],
                is_transpose=True,
                start=False,
                stop=True,
            )
            if pair == 0:
                nc.scalar.copy(out=s_sb[:, pair, :], in_=s_banks[pair][:, 0:P])
            else:
                nc.vector.tensor_copy(out=s_sb[:, pair, :], in_=s_banks[pair][:, 0:P])
            for odd in range(2):
                nc.sync.dma_start(out=s_rows[odd][:, pair, :], in_=s_sb[SETS * odd : SETS * odd + SETS, pair, :])
